import numpy as np
import ml_dtypes


def mxq(x, axis, fmt="e4m3"):
    dtype, down = {"e4m3": (ml_dtypes.float8_e4m3fn, 7), "e5m2": (ml_dtypes.float8_e5m2, 14)}[fmt]
    v = np.moveaxis(np.asarray(x, np.float32).astype(ml_dtypes.bfloat16).astype(np.float64), axis, -1)
    blocks = v.reshape(v.shape[:-1] + (-1, 32))
    amax = np.abs(blocks).max(-1, keepdims=True)
    byte = np.maximum(np.where(amax > 0, np.frexp(amax)[1] - 1 + 127, 0) - down, 1)
    scale = np.exp2(byte - 127.0)
    codes = (blocks / scale).astype(np.float32).astype(dtype).astype(np.float64)
    return np.moveaxis((codes * scale).reshape(v.shape), -1, axis)


WIDE = False


def mx_kscale(k):
    if not WIDE:
        return np.ones(k)
    levels = np.array([10, -10, 5, -5, 0])
    a = np.random.permutation(np.resize(levels, k // 512 * 4)).reshape(k // 512, 4)
    idx = np.arange(k)
    return np.exp2(a[idx // 512, idx % 128 // 32])


BF16 = ml_dtypes.bfloat16


def bf(x):
    return np.asarray(x, np.float32).astype(BF16)


def f64(x):
    return np.asarray(x).astype(np.float64)


B, T, D, DEPTH, F = 4, 128, 1024, 4, 256
L = 2 ** DEPTH
N = L - 1
LF = L * F


def sigmoid(v):
    return 1.0 / (1.0 + np.exp(-v))


def leaf_probs(c):
    probs = np.ones(c.shape[:-1] + (1,))
    for m in range(DEPTH):
        start = 2 ** m - 1
        cl = c[..., start:start + 2 ** m]
        probs = np.stack([probs * cl, probs * (1.0 - cl)], axis=-1)
        probs = probs.reshape(probs.shape[:-2] + (-1,))
    return probs


def setup_inputs():
    s = mx_kscale(D)
    t = mx_kscale(LF).reshape(L, F)
    return {"x": bf(np.random.standard_normal((B, T, D)) * s),
            "node_logits": bf(np.random.standard_normal((B, T, N)) * 1.5),
            "node_b": bf(np.random.standard_normal(N) * 0.5),
            "w1": bf(np.random.standard_normal((L, D, F)) / np.sqrt(D) / s[None, :, None] * t[:, None, :]),
            "b1": bf(np.random.standard_normal((L, F)) * 0.5 * t),
            "w2": bf(np.random.standard_normal((L, F, D)) * 2.0 / np.sqrt(F) / t[:, :, None])}


def reference(x, node_logits, node_b, w1, b1, w2):
    probs = leaf_probs(sigmoid(f64(node_logits) + f64(node_b)))
    w1f = f64(w1).transpose(1, 0, 2).reshape(D, LF)
    a = mxq(f64(x), 2, "e4m3") @ mxq(w1f, 0, "e4m3")
    h = np.maximum(a.reshape(B, T, L, F) + f64(b1), 0.0) * probs[..., None]
    return mxq(h.reshape(B, T, LF), 2, "e4m3") @ mxq(f64(w2).reshape(LF, D), 0, "e4m3")

@@ -1,0 +1,349 @@
+from contextlib import ExitStack
+
+import concourse.mybir as mybir
+from concourse.masks import make_identity
+
+F32 = mybir.dt.float32
+BF16 = mybir.dt.bfloat16
+U32 = mybir.dt.uint32
+U8 = mybir.dt.uint8
+FP8X4 = mybir.dt.float8_e4m3fn_x4
+ADD = mybir.AluOpType.add
+MULT = mybir.AluOpType.mult
+RELU = mybir.ActivationFunctionType.Relu
+SIGMOID = mybir.ActivationFunctionType.Sigmoid
+
+P = 128
+PACK = 4
+K_PASS = P * PACK
+TOKENS = 512
+TOKEN_BLOCKS = TOKENS // P
+D = 1024
+D_PASSES = D // K_PASS
+DEPTH = 4
+LEAVES = 2**DEPTH
+NODES = LEAVES - 1
+F = 256
+PAIRS = LEAVES * F // K_PASS
+HALF_P = P // 2
+E = 1024
+E_HALF = 512
+PIECES = 2 * PAIRS
+RUN = 4
+PSUM_BANKS = 8
+RAW1_BUFS = 4
+STORE_LAG = 2
+
+FLOPS = 2 * TOKENS * D * LEAVES * F + 2 * TOKENS * LEAVES * F * E
+
+
+def tile_fastfeedforwardnetwork_pa_kernel(tc, x, node_logits, node_b, w1, b1, w2, out):
+    nc = tc.nc
+    x_rows = x.flatten_outer_dims()
+    logit_rows = node_logits.flatten_outer_dims()
+    w2_rows = w2.flatten_outer_dims()
+    out_rows = out.flatten_outer_dims()
+
+    with ExitStack() as stack:
+        stack.enter_context(tc.manual_schedule())
+        keep = stack.enter_context(tc.tile_pool(name="keep", bufs=1))
+        raw1_pool = stack.enter_context(tc.tile_pool(name="raw1", bufs=RAW1_BUFS))
+        raw2_pool = stack.enter_context(tc.tile_pool(name="raw2", bufs=PAIRS))
+        w1_pool = stack.enter_context(tc.tile_pool(name="w1", bufs=2))
+        hidden_pool = stack.enter_context(tc.tile_pool(name="hidden", bufs=2))
+        psum = stack.enter_context(tc.psum_pool(name="psum", bufs=PSUM_BANKS))
+
+        identity = keep.tile([P, P], F32)
+        bias = keep.tile([P, PAIRS * PACK], F32)
+        leaf_rows = keep.tile([P, TOKENS], F32)
+        leaf_of_partition = keep.tile([P, LEAVES, HALF_P], F32)
+        probs = keep.tile([P, PAIRS, TOKENS], F32)
+        x_codes = keep.tile([P, D_PASSES, TOKENS], U32, align_bytes=64)
+        x_scales = keep.tile([P, D_PASSES, TOKENS], U8, align_bytes=64)
+        h_codes = keep.tile([P, PAIRS, TOKENS], U32, align_bytes=64)
+        h_scales = keep.tile([P, PAIRS, TOKENS], U8, align_bytes=64)
+
+        raw1 = {}
+        raw2 = {}
+        grouped1 = {}
+        mx1 = {}
+        grouped2 = {}
+        mx2 = {}
+        pre_banks = {}
+        gated = {}
+        hidden = {}
+        sums = {}
+
+        def load_w1(g):
+            raw = raw1_pool.tile([P, 2, D_PASSES, PACK, F], BF16, name="raw1")
+            nc.sync.dma_start(
+                out=raw[:].rearrange("p h c j f -> p h c (j f)"),
+                in_=w1[2 * g : 2 * g + 2].rearrange("h (c p j) f -> p h c (j f)", c=D_PASSES, p=P, j=PACK),
+            )
+            raw1[g] = raw
+
+        def load_w2(g):
+            raw = raw2_pool.tile([P, PACK, E], BF16, name="raw2")
+            nc.sync.dma_start(
+                out=raw[:].rearrange("p t e -> p (t e)"),
+                in_=w2_rows[g * K_PASS : (g + 1) * K_PASS, :].rearrange("(p t) e -> p (t e)", t=PACK),
+            )
+            raw2[g] = raw
+
+        def regroup_w1(g):
+            grouped = w1_pool.tile([P, D_PASSES, PACK, P, PACK], BF16, name="grouped1", align_bytes=64)
+            for c in range(D_PASSES):
+                nc.vector.tensor_copy(
+                    out=grouped[:, c, :, 0:HALF_P, :],
+                    in_=raw1[g][:, 0, c, :, :].rearrange("p j (m t) -> p t m j", t=PACK),
+                )
+                nc.scalar.copy(
+                    out=grouped[:, c, :, HALF_P:P, :],
+                    in_=raw1[g][:, 1, c, :, :].rearrange("p j (m t) -> p t m j", t=PACK),
+                )
+            grouped1[g] = grouped
+            if g + RAW1_BUFS < PAIRS:
+                load_w1(g + RAW1_BUFS)
+            if g + RAW1_BUFS == PAIRS - 1:
+                for later in range(PAIRS):
+                    load_w2(later)
+
+        def quantise_w1(g):
+            codes = w1_pool.tile([P, D_PASSES, K_PASS], U32, name="codes1", align_bytes=64)
+            scales = w1_pool.tile([P, D_PASSES, K_PASS], U8, name="scales1", align_bytes=64)
+            nc.vector.quantize_mx(
+                out=codes[:].rearrange("p c w -> p (c w)").bitcast(FP8X4),
+                scales=scales[:].rearrange("p c w -> p (c w)"),
+                in_=grouped1[g][:].rearrange("p c t m j -> p (c t m j)"),
+            )
+            mx1[g] = (codes, scales)
+
+        def first_matmul(g):
+            codes, scales = mx1[g]
+            banks = []
+            for t in range(PACK):
+                bank = psum.tile([P, TOKENS], F32, name="pre", tag="bank")
+                block = slice(t * P, (t + 1) * P)
+                for c in range(D_PASSES):
+                    nc.tensor.matmul_mx(
+                        out=bank[:],
+                        lhsT=codes[:, c, block].bitcast(FP8X4),
+                        lhsT_scale=scales[:, c, block],
+                        rhs=x_codes[:, c, :].bitcast(FP8X4),
+                        rhs_scale=x_scales[:, c, :],
+                        start=(c == 0),
+                        stop=(c == D_PASSES - 1),
+                    )
+                banks.append(bank)
+            pre_banks[g] = banks
+
+        def spread_probs(g):
+            bank = psum.tile([P, TOKENS], F32, name="spread", tag="bank")
+            nc.tensor.matmul(
+                out=bank[:],
+                lhsT=leaf_of_partition[:, 2 * g : 2 * g + 2, :].rearrange("p l i -> p (l i)"),
+                rhs=leaf_rows[:],
+                start=True,
+                stop=True,
+            )
+            nc.scalar.copy(out=probs[:, g, :], in_=bank[:])
+
+        def bias_and_gate(g):
+            z = hidden_pool.tile([P, PACK, TOKENS], BF16, name="gated")
+            for t in range(PACK):
+                nc.vector.scalar_tensor_tensor(
+                    out=z[:, t, :],
+                    in0=pre_banks[g][t][:],
+                    scalar=bias[:, g * PACK + t : g * PACK + t + 1],
+                    in1=probs[:, g, :],
+                    op0=ADD,
+                    op1=MULT,
+                )
+            gated[g] = z
+
+        def relu_regroup(g):
+            h = hidden_pool.tile([P, TOKENS, PACK], BF16, name="hidden", align_bytes=64)
+            nc.scalar.activation(
+                out=h[:].rearrange("p (n i) t -> p n t i", i=RUN),
+                in_=gated[g][:].rearrange("p t (n i) -> p n t i", i=RUN),
+                func=RELU,
+            )
+            hidden[g] = h
+
+        def quantise_h(g):
+            nc.vector.quantize_mx(
+                out=h_codes[:, g, :].bitcast(FP8X4),
+                scales=h_scales[:, g, :],
+                in_=hidden[g][:].rearrange("p n t -> p (n t)"),
+            )
+
+        with tc.tile_pool(name="setup", bufs=1) as setup:
+            logits = setup.tile([P, TOKEN_BLOCKS, NODES], BF16)
+            nc.scalar.dma_start(out=logits[:], in_=logit_rows.rearrange("(b p) n -> p b n", p=P))
+            node_bias = setup.tile([P, NODES], BF16)
+            nc.scalar.dma_start(out=node_bias[:], in_=node_b.partition_broadcast(P))
+            b1_bf = setup.tile([P, PAIRS, PACK], BF16)
+            nc.scalar.dma_start(
+                out=b1_bf[:],
+                in_=b1.rearrange("l f -> (l f)").rearrange("(g p t) -> p g t", g=PAIRS, p=P),
+            )
+            load_w1(0)
+            x_blocks = []
+            for b in range(TOKEN_BLOCKS):
+                x_block = setup.tile([P, D], BF16, name="x%d" % b)
+                nc.sync.dma_start(out=x_block[:], in_=x_rows[b * P : (b + 1) * P, :])
+                x_blocks.append(x_block)
+            for g in range(1, RAW1_BUFS):
+                load_w1(g)
+
+            make_identity(nc, identity[:])
+            probs_by_token = setup.tile([P, TOKEN_BLOCKS, P], F32)
+            nc.gpsimd.memset(probs_by_token[:], 0.0)
+            gate_in = setup.tile([P, TOKEN_BLOCKS, NODES], F32)
+            nc.vector.tensor_tensor(
+                out=gate_in[:],
+                in0=logits[:],
+                in1=node_bias[:].unsqueeze(1).to_broadcast([P, TOKEN_BLOCKS, NODES]),
+                op=ADD,
+            )
+            gates = setup.tile([P, TOKEN_BLOCKS, NODES, 2], F32)
+            nc.scalar.activation(out=gates[:, :, :, 0], in_=gate_in[:], func=SIGMOID)
+            nc.scalar.activation(out=gates[:, :, :, 1], in_=gate_in[:], func=SIGMOID, scale=-1.0)
+            level = gates[:, :, 0, :]
+            for m in range(1, DEPTH):
+                nodes = 2**m
+                if m < DEPTH - 1:
+                    children = setup.tile([P, TOKEN_BLOCKS, 2 * nodes], F32, name="level%d" % m)[:]
+                else:
+                    children = probs_by_token[:, :, 0:LEAVES]
+                nc.vector.tensor_tensor(
+                    out=children.rearrange("p b (n s) -> p b n s", s=2),
+                    in0=level.unsqueeze(3).to_broadcast([P, TOKEN_BLOCKS, nodes, 2]),
+                    in1=gates[:, :, nodes - 1 : 2 * nodes - 1, :],
+                    op=MULT,
+                )
+                level = children
+            nc.vector.tensor_copy(
+                out=leaf_of_partition[:],
+                in_=identity[:, 0:LEAVES].unsqueeze(2).to_broadcast([P, LEAVES, HALF_P]),
+            )
+            nc.vector.tensor_copy(out=bias[:], in_=b1_bf[:].rearrange("p g t -> p (g t)"))
+            turned = psum.tile([P, TOKEN_BLOCKS, P], F32, name="turned", tag="bank")
+            for b in range(TOKEN_BLOCKS):
+                nc.tensor.transpose(turned[:, b, :], probs_by_token[:, b, :], identity[:])
+            nc.scalar.copy(out=leaf_rows[:], in_=turned[:].rearrange("p b n -> p (b n)"))
+
+            regroup_w1(0)
+
+            x_grouped = setup.tile([P, D_PASSES * TOKENS * PACK], BF16, align_bytes=64)
+            x_grouped_words = x_grouped[:].bitcast(F32).rearrange("p (c n u) -> p c n u", c=D_PASSES, u=2)
+            for b in range(TOKEN_BLOCKS):
+                words = x_blocks[b][:].bitcast(F32)
+                x_turned = psum.tile([P, D_PASSES, 2, P], F32, name="x_turned", tag="bank")
+                for c in range(D_PASSES):
+                    for u in range(2):
+                        first = c * (K_PASS // 2) + u
+                        nc.tensor.transpose(
+                            x_turned[:, c, u, :], words[:, first : (c + 1) * (K_PASS // 2) : 2], identity[:]
+                        )
+                if b < TOKEN_BLOCKS // 2:
+                    copy_out = nc.vector.tensor_copy
+                else:
+                    copy_out = nc.scalar.copy
+                copy_out(
+                    out=x_grouped_words[:, :, b * P : (b + 1) * P, :],
+                    in_=x_turned[:].rearrange("p c u n -> p c n u"),
+                )
+            spread_probs(0)
+            quantise_w1(0)
+            nc.vector.quantize_mx(
+                out=x_codes[:].rearrange("p c n -> p (c n)").bitcast(FP8X4),
+                scales=x_scales[:].rearrange("p c n -> p (c n)"),
+                in_=x_grouped[:],
+            )
+            regroup_w1(1)
+
+        w2_pool = stack.enter_context(tc.tile_pool(name="w2", bufs=4))
+        out_pool = stack.enter_context(tc.tile_pool(name="out", bufs=TOKEN_BLOCKS))
+
+        def regroup_w2(q):
+            half, g = divmod(q, PAIRS)
+            grouped = w2_pool.tile([P, E_HALF, PACK], BF16, name="grouped2", align_bytes=64)
+            cut = E_HALF // 2
+            nc.vector.tensor_copy(
+                out=grouped[:, 0:cut, :].rearrange("p (n i) t -> p n t i", i=RUN),
+                in_=raw2[g][:, :, half * E_HALF : half * E_HALF + cut].rearrange("p t (n i) -> p n t i", i=RUN),
+            )
+            nc.scalar.copy(
+                out=grouped[:, cut:E_HALF, :].rearrange("p (n i) t -> p n t i", i=RUN),
+                in_=raw2[g][:, :, half * E_HALF + cut : (half + 1) * E_HALF].rearrange("p t (n i) -> p n t i", i=RUN),
+            )
+            grouped2[q] = grouped
+
+        def quantise_w2(q):
+            codes = w2_pool.tile([P, E_HALF], U32, name="codes2", align_bytes=64)
+            scales = w2_pool.tile([P, E_HALF], U8, name="scales2", align_bytes=64)
+            nc.vector.quantize_mx(
+                out=codes[:].bitcast(FP8X4),
+                scales=scales[:],
+                in_=grouped2[q][:].rearrange("p e t -> p (e t)"),
+            )
+            mx2[q] = (codes, scales)
+
+        def second_matmul(q):
+            half, g = divmod(q, PAIRS)
+            codes, scales = mx2[q]
+            for b in range(TOKEN_BLOCKS):
+                if g == 0:
+                    sums[(half, b)] = psum.tile([P, E_HALF], F32, name="sums", tag="bank")
+                block = slice(b * P, (b + 1) * P)
+                nc.tensor.matmul_mx(
+                    out=sums[(half, b)][:],
+                    lhsT=h_codes[:, g, block].bitcast(FP8X4),
+                    lhsT_scale=h_scales[:, g, block],
+                    rhs=codes[:].bitcast(FP8X4),
+                    rhs_scale=scales[:],
+                    start=(g == 0),
+                    stop=(g == PAIRS - 1),
+                )
+
+        def store_half(half):
+            for b in range(TOKEN_BLOCKS):
+                result = out_pool.tile([P, E_HALF], F32, name="result")
+                if b % 2 == 0:
+                    nc.vector.tensor_copy(out=result[:], in_=sums[(half, b)][:])
+                else:
+                    nc.scalar.copy(out=result[:], in_=sums[(half, b)][:])
+                nc.sync.dma_start(
+                    out=out_rows[b * P : (b + 1) * P, half * E_HALF : (half + 1) * E_HALF], in_=result[:]
+                )
+
+        for g in range(PAIRS):
+            first_matmul(g)
+            if g + 1 < PAIRS:
+                spread_probs(g + 1)
+            bias_and_gate(g)
+            if g + 1 < PAIRS:
+                quantise_w1(g + 1)
+            else:
+                quantise_w2(0)
+                quantise_w2(1)
+            if g + 2 < PAIRS:
+                regroup_w1(g + 2)
+            else:
+                regroup_w2(2 * (g + 2 - PAIRS))
+                regroup_w2(2 * (g + 2 - PAIRS) + 1)
+            relu_regroup(g)
+            if g > 0:
+                quantise_h(g - 1)
+        quantise_h(PAIRS - 1)
+
+        for q in range(PIECES):
+            second_matmul(q)
+            if q + 2 < PIECES:
+                quantise_w2(q + 2)
+            if q + 4 < PIECES:
+                regroup_w2(q + 4)
+            if q == PAIRS - 1 + STORE_LAG:
+                store_half(0)
+        store_half(1)

@@ -94,12 +94,12 @@ def tile_fastfeedforwardnetwork_pa_kernel(tc, x, node_logits, node_b, w1, b1, w2
             grouped = w1_pool.tile([P, D_PASSES, PACK, P, PACK], BF16, name="grouped1", align_bytes=64)
             for c in range(D_PASSES):
                 nc.vector.tensor_copy(
-                    out=grouped[:, c, :, 0:HALF_P, :],
-                    in_=raw1[g][:, 0, c, :, :].rearrange("p j (m t) -> p t m j", t=PACK),
+                    out=grouped[:, c, :, 0:HALF_P, :].rearrange("p t m j -> p m j t"),
+                    in_=raw1[g][:, 0, c, :, :].rearrange("p j (m t) -> p m j t", t=PACK),
                 )
                 nc.scalar.copy(
-                    out=grouped[:, c, :, HALF_P:P, :],
-                    in_=raw1[g][:, 1, c, :, :].rearrange("p j (m t) -> p t m j", t=PACK),
+                    out=grouped[:, c, :, HALF_P:P, :].rearrange("p t m j -> p m j t"),
+                    in_=raw1[g][:, 1, c, :, :].rearrange("p j (m t) -> p m j t", t=PACK),
                 )
             grouped1[g] = grouped
             if g + RAW1_BUFS < PAIRS:

@@ -31,7 +31,8 @@ E_HALF = 512
 PIECES = 2 * PAIRS
 RUN = 4
 PSUM_BANKS = 8
-RAW1_BUFS = 4
+W1_PIECES = PAIRS * D_PASSES
+RAW1_BUFS = 8
 STORE_LAG = 2
 
 FLOPS = 2 * TOKENS * D * LEAVES * F + 2 * TOKENS * LEAVES * F * E
@@ -45,11 +46,10 @@ def tile_fastfeedforwardnetwork_pa_kernel(tc, x, node_logits, node_b, w1, b1, w2
     out_rows = out.flatten_outer_dims()
 
     with ExitStack() as stack:
-        stack.enter_context(tc.manual_schedule())
         keep = stack.enter_context(tc.tile_pool(name="keep", bufs=1))
         raw1_pool = stack.enter_context(tc.tile_pool(name="raw1", bufs=RAW1_BUFS))
         raw2_pool = stack.enter_context(tc.tile_pool(name="raw2", bufs=PAIRS))
-        w1_pool = stack.enter_context(tc.tile_pool(name="w1", bufs=2))
+        w1_pool = stack.enter_context(tc.tile_pool(name="w1", bufs=4))
         hidden_pool = stack.enter_context(tc.tile_pool(name="hidden", bufs=2))
         psum = stack.enter_context(tc.psum_pool(name="psum", bufs=PSUM_BANKS))
 
@@ -74,13 +74,14 @@ def tile_fastfeedforwardnetwork_pa_kernel(tc, x, node_logits, node_b, w1, b1, w2
         hidden = {}
         sums = {}
 
-        def load_w1(g):
-            raw = raw1_pool.tile([P, 2, D_PASSES, PACK, F], BF16, name="raw1")
+        def load_w1(k):
+            g, c = divmod(k, D_PASSES)
+            raw = raw1_pool.tile([P, 2, PACK, F], BF16, name="raw1")
             nc.sync.dma_start(
-                out=raw[:].rearrange("p h c j f -> p h c (j f)"),
-                in_=w1[2 * g : 2 * g + 2].rearrange("h (c p j) f -> p h c (j f)", c=D_PASSES, p=P, j=PACK),
+                out=raw[:].rearrange("p h j f -> p h (j f)"),
+                in_=w1[2 * g : 2 * g + 2, c * K_PASS : (c + 1) * K_PASS, :].rearrange("h (p j) f -> p h (j f)", j=PACK),
             )
-            raw1[g] = raw
+            raw1[k] = raw
 
         def load_w2(g):
             raw = raw2_pool.tile([P, PACK, E], BF16, name="raw2")
@@ -90,45 +91,44 @@ def tile_fastfeedforwardnetwork_pa_kernel(tc, x, node_logits, node_b, w1, b1, w2
             )
             raw2[g] = raw
 
-        def regroup_w1(g):
-            grouped = w1_pool.tile([P, D_PASSES, PACK, P, PACK], BF16, name="grouped1", align_bytes=64)
-            for c in range(D_PASSES):
-                nc.vector.tensor_copy(
-                    out=grouped[:, c, :, 0:HALF_P, :].rearrange("p t m j -> p m j t"),
-                    in_=raw1[g][:, 0, c, :, :].rearrange("p j (m t) -> p m j t", t=PACK),
-                )
-                nc.scalar.copy(
-                    out=grouped[:, c, :, HALF_P:P, :].rearrange("p t m j -> p m j t"),
-                    in_=raw1[g][:, 1, c, :, :].rearrange("p j (m t) -> p m j t", t=PACK),
-                )
-            grouped1[g] = grouped
-            if g + RAW1_BUFS < PAIRS:
-                load_w1(g + RAW1_BUFS)
-            if g + RAW1_BUFS == PAIRS - 1:
+        def regroup_w1(k):
+            grouped = w1_pool.tile([P, PACK, P, PACK], BF16, name="grouped1", align_bytes=64)
+            nc.vector.tensor_copy(
+                out=grouped[:, :, 0:HALF_P, :].rearrange("p t m j -> p m j t"),
+                in_=raw1[k][:, 0, :, :].rearrange("p j (m t) -> p m j t", t=PACK),
+            )
+            nc.scalar.copy(
+                out=grouped[:, :, HALF_P:P, :].rearrange("p t m j -> p m j t"),
+                in_=raw1[k][:, 1, :, :].rearrange("p j (m t) -> p m j t", t=PACK),
+            )
+            grouped1[k] = grouped
+            if k + RAW1_BUFS < W1_PIECES:
+                load_w1(k + RAW1_BUFS)
+            if k + RAW1_BUFS == W1_PIECES - 1:
                 for later in range(PAIRS):
                     load_w2(later)
 
-        def quantise_w1(g):
-            codes = w1_pool.tile([P, D_PASSES, K_PASS], U32, name="codes1", align_bytes=64)
-            scales = w1_pool.tile([P, D_PASSES, K_PASS], U8, name="scales1", align_bytes=64)
+        def quantise_w1(k):
+            codes = w1_pool.tile([P, K_PASS], U32, name="codes1", align_bytes=64)
+            scales = w1_pool.tile([P, K_PASS], U8, name="scales1", align_bytes=64)
             nc.vector.quantize_mx(
-                out=codes[:].rearrange("p c w -> p (c w)").bitcast(FP8X4),
-                scales=scales[:].rearrange("p c w -> p (c w)"),
-                in_=grouped1[g][:].rearrange("p c t m j -> p (c t m j)"),
+                out=codes[:].bitcast(FP8X4),
+                scales=scales[:],
+                in_=grouped1[k][:].rearrange("p t m j -> p (t m j)"),
             )
-            mx1[g] = (codes, scales)
+            mx1[k] = (codes, scales)
 
         def first_matmul(g):
-            codes, scales = mx1[g]
             banks = []
             for t in range(PACK):
                 bank = psum.tile([P, TOKENS], F32, name="pre", tag="bank")
                 block = slice(t * P, (t + 1) * P)
                 for c in range(D_PASSES):
+                    codes, scales = mx1[g * D_PASSES + c]
                     nc.tensor.matmul_mx(
                         out=bank[:],
-                        lhsT=codes[:, c, block].bitcast(FP8X4),
-                        lhsT_scale=scales[:, c, block],
+                        lhsT=codes[:, block].bitcast(FP8X4),
+                        lhsT_scale=scales[:, block],
                         rhs=x_codes[:, c, :].bitcast(FP8X4),
                         rhs_scale=x_scales[:, c, :],
                         start=(c == 0),
@@ -188,13 +188,14 @@ def tile_fastfeedforwardnetwork_pa_kernel(tc, x, node_logits, node_b, w1, b1, w2
                 in_=b1.rearrange("l f -> (l f)").rearrange("(g p t) -> p g t", g=PAIRS, p=P),
             )
             load_w1(0)
+            load_w1(1)
             x_blocks = []
             for b in range(TOKEN_BLOCKS):
                 x_block = setup.tile([P, D], BF16, name="x%d" % b)
                 nc.sync.dma_start(out=x_block[:], in_=x_rows[b * P : (b + 1) * P, :])
                 x_blocks.append(x_block)
-            for g in range(1, RAW1_BUFS):
-                load_w1(g)
+            for k in range(2, RAW1_BUFS):
+                load_w1(k)
 
             make_identity(nc, identity[:])
             probs_by_token = setup.tile([P, TOKEN_BLOCKS, P], F32)
@@ -234,6 +235,7 @@ def tile_fastfeedforwardnetwork_pa_kernel(tc, x, node_logits, node_b, w1, b1, w2
             nc.scalar.copy(out=leaf_rows[:], in_=turned[:].rearrange("p b n -> p (b n)"))
 
             regroup_w1(0)
+            regroup_w1(1)
 
             x_grouped = setup.tile([P, D_PASSES * TOKENS * PACK], BF16, align_bytes=64)
             x_grouped_words = x_grouped[:].bitcast(F32).rearrange("p (c n u) -> p c n u", c=D_PASSES, u=2)
@@ -256,12 +258,15 @@ def tile_fastfeedforwardnetwork_pa_kernel(tc, x, node_logits, node_b, w1, b1, w2
                 )
             spread_probs(0)
             quantise_w1(0)
-            nc.vector.quantize_mx(
-                out=x_codes[:].rearrange("p c n -> p (c n)").bitcast(FP8X4),
-                scales=x_scales[:].rearrange("p c n -> p (c n)"),
-                in_=x_grouped[:],
-            )
-            regroup_w1(1)
+            quantise_w1(1)
+            for c in range(D_PASSES):
+                nc.vector.quantize_mx(
+                    out=x_codes[:, c, :].bitcast(FP8X4),
+                    scales=x_scales[:, c, :],
+                    in_=x_grouped[:, c * TOKENS * PACK : (c + 1) * TOKENS * PACK],
+                )
+            regroup_w1(2)
+            regroup_w1(3)
 
         w2_pool = stack.enter_context(tc.tile_pool(name="w2", bufs=4))
         out_pool = stack.enter_context(tc.tile_pool(name="out", bufs=TOKEN_BLOCKS))
@@ -324,12 +329,14 @@ def tile_fastfeedforwardnetwork_pa_kernel(tc, x, node_logits, node_b, w1, b1, w2
                 spread_probs(g + 1)
             bias_and_gate(g)
             if g + 1 < PAIRS:
-                quantise_w1(g + 1)
+                quantise_w1(2 * g + 2)
+                quantise_w1(2 * g + 3)
             else:
                 quantise_w2(0)
                 quantise_w2(1)
             if g + 2 < PAIRS:
-                regroup_w1(g + 2)
+                regroup_w1(2 * g + 4)
+                regroup_w1(2 * g + 5)
             else:
                 regroup_w2(2 * (g + 2 - PAIRS))
                 regroup_w2(2 * (g + 2 - PAIRS) + 1)

@@ -93,9 +93,18 @@ def tile_fastfeedforwardnetwork_pa_kernel(tc, x, node_logits, node_b, w1, b1, w2
 
         def regroup_w1(k):
             grouped = w1_pool.tile([P, PACK, P, PACK], BF16, name="grouped1", align_bytes=64)
+            shared = HALF_P // 2
             nc.vector.tensor_copy(
-                out=grouped[:, :, 0:HALF_P, :].rearrange("p t m j -> p m j t"),
-                in_=raw1[k][:, 0, :, :].rearrange("p j (m t) -> p m j t", t=PACK),
+                out=grouped[:, :, 0:shared, :].rearrange("p t m j -> p m j t"),
+                in_=raw1[k][:, 0, :, 0 : shared * PACK].rearrange("p j (m t) -> p m j t", t=PACK),
+            )
+            nc.gpsimd.tensor_scalar(
+                out=grouped[:, :, shared:HALF_P, :].rearrange("p t m j -> p m j t"),
+                in0=raw1[k][:, 0, :, shared * PACK : F].rearrange("p j (m t) -> p m j t", t=PACK),
+                scalar1=1.0,
+                scalar2=0.0,
+                op0=MULT,
+                op1=ADD,
             )
             nc.scalar.copy(
                 out=grouped[:, :, HALF_P:P, :].rearrange("p t m j -> p m j t"),

@@ -32,8 +32,8 @@ PIECES = 2 * PAIRS
 RUN = 4
 PSUM_BANKS = 8
 W1_PIECES = PAIRS * D_PASSES
+GPSIMD_CUT = 320
 RAW1_BUFS = 8
-STORE_LAG = 2
 
 FLOPS = 2 * TOKENS * D * LEAVES * F + 2 * TOKENS * LEAVES * F * E
 
@@ -46,6 +46,7 @@ def tile_fastfeedforwardnetwork_pa_kernel(tc, x, node_logits, node_b, w1, b1, w2
     out_rows = out.flatten_outer_dims()
 
     with ExitStack() as stack:
+        stack.enter_context(tc.manual_schedule())
         keep = stack.enter_context(tc.tile_pool(name="keep", bufs=1))
         raw1_pool = stack.enter_context(tc.tile_pool(name="raw1", bufs=RAW1_BUFS))
         raw2_pool = stack.enter_context(tc.tile_pool(name="raw2", bufs=PAIRS))
@@ -55,8 +56,7 @@ def tile_fastfeedforwardnetwork_pa_kernel(tc, x, node_logits, node_b, w1, b1, w2
 
         identity = keep.tile([P, P], F32)
         bias = keep.tile([P, PAIRS * PACK], F32)
-        leaf_rows = keep.tile([P, TOKENS], F32)
-        leaf_of_partition = keep.tile([P, LEAVES, HALF_P], F32)
+        probs_by_token = keep.tile([P, TOKEN_BLOCKS, LEAVES], F32)
         probs = keep.tile([P, PAIRS, TOKENS], F32)
         x_codes = keep.tile([P, D_PASSES, TOKENS], U32, align_bytes=64)
         x_scales = keep.tile([P, D_PASSES, TOKENS], U8, align_bytes=64)
@@ -69,6 +69,7 @@ def tile_fastfeedforwardnetwork_pa_kernel(tc, x, node_logits, node_b, w1, b1, w2
         mx1 = {}
         grouped2 = {}
         mx2 = {}
+        repeated = {}
         pre_banks = {}
         gated = {}
         hidden = {}
@@ -91,31 +92,13 @@ def tile_fastfeedforwardnetwork_pa_kernel(tc, x, node_logits, node_b, w1, b1, w2
             )
             raw2[g] = raw
 
-        def regroup_w1(k):
-            grouped = w1_pool.tile([P, PACK, P, PACK], BF16, name="grouped1", align_bytes=64)
-            shared = HALF_P // 2
-            nc.vector.tensor_copy(
-                out=grouped[:, :, 0:shared, :].rearrange("p t m j -> p m j t"),
-                in_=raw1[k][:, 0, :, 0 : shared * PACK].rearrange("p j (m t) -> p m j t", t=PACK),
+        def regroup_w1(k, h, copy):
+            if k not in grouped1:
+                grouped1[k] = w1_pool.tile([P, PACK, P, PACK], BF16, name="grouped1", align_bytes=64)
+            copy(
+                out=grouped1[k][:, :, h * HALF_P : (h + 1) * HALF_P, :].rearrange("p t m j -> p m j t"),
+                in_=raw1[k][:, h, :, :].rearrange("p j (m t) -> p m j t", t=PACK),
             )
-            nc.gpsimd.tensor_scalar(
-                out=grouped[:, :, shared:HALF_P, :].rearrange("p t m j -> p m j t"),
-                in0=raw1[k][:, 0, :, shared * PACK : F].rearrange("p j (m t) -> p m j t", t=PACK),
-                scalar1=1.0,
-                scalar2=0.0,
-                op0=MULT,
-                op1=ADD,
-            )
-            nc.scalar.copy(
-                out=grouped[:, :, HALF_P:P, :].rearrange("p t m j -> p m j t"),
-                in_=raw1[k][:, 1, :, :].rearrange("p j (m t) -> p m j t", t=PACK),
-            )
-            grouped1[k] = grouped
-            if k + RAW1_BUFS < W1_PIECES:
-                load_w1(k + RAW1_BUFS)
-            if k + RAW1_BUFS == W1_PIECES - 1:
-                for later in range(PAIRS):
-                    load_w2(later)
 
         def quantise_w1(k):
             codes = w1_pool.tile([P, K_PASS], U32, name="codes1", align_bytes=64)
@@ -146,16 +129,23 @@ def tile_fastfeedforwardnetwork_pa_kernel(tc, x, node_logits, node_b, w1, b1, w2
                 banks.append(bank)
             pre_banks[g] = banks
 
-        def spread_probs(g):
-            bank = psum.tile([P, TOKENS], F32, name="spread", tag="bank")
-            nc.tensor.matmul(
-                out=bank[:],
-                lhsT=leaf_of_partition[:, 2 * g : 2 * g + 2, :].rearrange("p l i -> p (l i)"),
-                rhs=leaf_rows[:],
-                start=True,
-                stop=True,
+        def repeat_probs(g):
+            rep = hidden_pool.tile([P, TOKEN_BLOCKS, P], F32, name="repeated")
+            nc.gpsimd.tensor_scalar(
+                out=rep[:].rearrange("p b (l i) -> p b l i", l=2),
+                in0=probs_by_token[:, :, 2 * g : 2 * g + 2].unsqueeze(3).to_broadcast([P, TOKEN_BLOCKS, 2, HALF_P]),
+                scalar1=1.0,
+                scalar2=0.0,
+                op0=MULT,
+                op1=ADD,
             )
-            nc.scalar.copy(out=probs[:, g, :], in_=bank[:])
+            repeated[g] = rep
+
+        def spread_probs(g):
+            bank = psum.tile([P, TOKEN_BLOCKS, P], F32, name="spread", tag="bank")
+            for b in range(TOKEN_BLOCKS):
+                nc.tensor.transpose(bank[:, b, :], repeated[g][:, b, :], identity[:])
+            nc.scalar.copy(out=probs[:, g, :], in_=bank[:].rearrange("p b n -> p (b n)"))
 
         def bias_and_gate(g):
             z = hidden_pool.tile([P, PACK, TOKENS], BF16, name="gated")
@@ -172,10 +162,10 @@ def tile_fastfeedforwardnetwork_pa_kernel(tc, x, node_logits, node_b, w1, b1, w2
 
         def relu_regroup(g):
             h = hidden_pool.tile([P, TOKENS, PACK], BF16, name="hidden", align_bytes=64)
-            nc.scalar.activation(
+            nc.vector.tensor_scalar_max(
                 out=h[:].rearrange("p (n i) t -> p n t i", i=RUN),
-                in_=gated[g][:].rearrange("p t (n i) -> p n t i", i=RUN),
-                func=RELU,
+                in0=gated[g][:].rearrange("p t (n i) -> p n t i", i=RUN),
+                scalar1=0.0,
             )
             hidden[g] = h
 
@@ -187,6 +177,8 @@ def tile_fastfeedforwardnetwork_pa_kernel(tc, x, node_logits, node_b, w1, b1, w2
             )
 
         with tc.tile_pool(name="setup", bufs=1) as setup:
+            warm = setup.tile([P, 1], F32)
+            nc.vector.memset(warm[:], 0.0)
             logits = setup.tile([P, TOKEN_BLOCKS, NODES], BF16)
             nc.scalar.dma_start(out=logits[:], in_=logit_rows.rearrange("(b p) n -> p b n", p=P))
             node_bias = setup.tile([P, NODES], BF16)
@@ -196,19 +188,26 @@ def tile_fastfeedforwardnetwork_pa_kernel(tc, x, node_logits, node_b, w1, b1, w2
                 out=b1_bf[:],
                 in_=b1.rearrange("l f -> (l f)").rearrange("(g p t) -> p g t", g=PAIRS, p=P),
             )
+            nc.scalar.activation(out=warm[:], in_=warm[:], func=SIGMOID)
+            make_identity(nc, identity[:])
             load_w1(0)
-            load_w1(1)
             x_blocks = []
             for b in range(TOKEN_BLOCKS):
                 x_block = setup.tile([P, D], BF16, name="x%d" % b)
                 nc.sync.dma_start(out=x_block[:], in_=x_rows[b * P : (b + 1) * P, :])
                 x_blocks.append(x_block)
-            for k in range(2, RAW1_BUFS):
+            for k in (1, 2, 3):
                 load_w1(k)
+            load_w2(0)
+            load_w1(4)
+            load_w1(5)
+            load_w2(1)
+            load_w1(6)
+            load_w1(7)
 
-            make_identity(nc, identity[:])
-            probs_by_token = setup.tile([P, TOKEN_BLOCKS, P], F32)
-            nc.gpsimd.memset(probs_by_token[:], 0.0)
+            regroup_w1(0, 0, nc.vector.tensor_copy)
+            regroup_w1(0, 1, nc.scalar.copy)
+
             gate_in = setup.tile([P, TOKEN_BLOCKS, NODES], F32)
             nc.vector.tensor_tensor(
                 out=gate_in[:],
@@ -219,36 +218,25 @@ def tile_fastfeedforwardnetwork_pa_kernel(tc, x, node_logits, node_b, w1, b1, w2
             gates = setup.tile([P, TOKEN_BLOCKS, NODES, 2], F32)
             nc.scalar.activation(out=gates[:, :, :, 0], in_=gate_in[:], func=SIGMOID)
             nc.scalar.activation(out=gates[:, :, :, 1], in_=gate_in[:], func=SIGMOID, scale=-1.0)
-            level = gates[:, :, 0, :]
-            for m in range(1, DEPTH):
+
+            def tree_level(m, level):
                 nodes = 2**m
                 if m < DEPTH - 1:
                     children = setup.tile([P, TOKEN_BLOCKS, 2 * nodes], F32, name="level%d" % m)[:]
                 else:
-                    children = probs_by_token[:, :, 0:LEAVES]
+                    children = probs_by_token[:]
                 nc.vector.tensor_tensor(
                     out=children.rearrange("p b (n s) -> p b n s", s=2),
                     in0=level.unsqueeze(3).to_broadcast([P, TOKEN_BLOCKS, nodes, 2]),
                     in1=gates[:, :, nodes - 1 : 2 * nodes - 1, :],
                     op=MULT,
                 )
-                level = children
-            nc.vector.tensor_copy(
-                out=leaf_of_partition[:],
-                in_=identity[:, 0:LEAVES].unsqueeze(2).to_broadcast([P, LEAVES, HALF_P]),
-            )
-            nc.vector.tensor_copy(out=bias[:], in_=b1_bf[:].rearrange("p g t -> p (g t)"))
-            turned = psum.tile([P, TOKEN_BLOCKS, P], F32, name="turned", tag="bank")
-            for b in range(TOKEN_BLOCKS):
-                nc.tensor.transpose(turned[:, b, :], probs_by_token[:, b, :], identity[:])
-            nc.scalar.copy(out=leaf_rows[:], in_=turned[:].rearrange("p b n -> p (b n)"))
-
-            regroup_w1(0)
-            regroup_w1(1)
+                return children
 
             x_grouped = setup.tile([P, D_PASSES * TOKENS * PACK], BF16, align_bytes=64)
             x_grouped_words = x_grouped[:].bitcast(F32).rearrange("p (c n u) -> p c n u", c=D_PASSES, u=2)
-            for b in range(TOKEN_BLOCKS):
+
+            def turn_x(b, copy):
                 words = x_blocks[b][:].bitcast(F32)
                 x_turned = psum.tile([P, D_PASSES, 2, P], F32, name="x_turned", tag="bank")
                 for c in range(D_PASSES):
@@ -257,42 +245,61 @@ def tile_fastfeedforwardnetwork_pa_kernel(tc, x, node_logits, node_b, w1, b1, w2
                         nc.tensor.transpose(
                             x_turned[:, c, u, :], words[:, first : (c + 1) * (K_PASS // 2) : 2], identity[:]
                         )
-                if b < TOKEN_BLOCKS // 2:
-                    copy_out = nc.vector.tensor_copy
-                else:
-                    copy_out = nc.scalar.copy
-                copy_out(
+                copy(
                     out=x_grouped_words[:, :, b * P : (b + 1) * P, :],
                     in_=x_turned[:].rearrange("p c u n -> p c n u"),
                 )
-            spread_probs(0)
+
             quantise_w1(0)
-            quantise_w1(1)
+            level = tree_level(1, gates[:, :, 0, :])
+            turn_x(0, nc.vector.tensor_copy)
+            level = tree_level(2, level)
+            turn_x(1, nc.scalar.copy)
+            turn_x(2, nc.vector.tensor_copy)
+            tree_level(3, level)
+            repeat_probs(0)
+            repeat_probs(1)
+            turn_x(3, nc.scalar.copy)
+            regroup_w1(1, 0, nc.vector.tensor_copy)
+            regroup_w1(1, 1, nc.scalar.copy)
             for c in range(D_PASSES):
                 nc.vector.quantize_mx(
                     out=x_codes[:, c, :].bitcast(FP8X4),
                     scales=x_scales[:, c, :],
                     in_=x_grouped[:, c * TOKENS * PACK : (c + 1) * TOKENS * PACK],
                 )
-            regroup_w1(2)
-            regroup_w1(3)
+            spread_probs(0)
+            quantise_w1(1)
+            nc.vector.tensor_copy(out=bias[:], in_=b1_bf[:].rearrange("p g t -> p (g t)"))
+            first_matmul(0)
+            for k in (2, 3):
+                regroup_w1(k, 0, nc.vector.tensor_copy)
+                regroup_w1(k, 1, nc.scalar.copy)
 
         w2_pool = stack.enter_context(tc.tile_pool(name="w2", bufs=4))
         out_pool = stack.enter_context(tc.tile_pool(name="out", bufs=TOKEN_BLOCKS))
 
-        def regroup_w2(q):
+        def regroup_w2(q, first, last, copy):
             half, g = divmod(q, PAIRS)
-            grouped = w2_pool.tile([P, E_HALF, PACK], BF16, name="grouped2", align_bytes=64)
-            cut = E_HALF // 2
-            nc.vector.tensor_copy(
-                out=grouped[:, 0:cut, :].rearrange("p (n i) t -> p n t i", i=RUN),
-                in_=raw2[g][:, :, half * E_HALF : half * E_HALF + cut].rearrange("p t (n i) -> p n t i", i=RUN),
+            if q not in grouped2:
+                grouped2[q] = w2_pool.tile([P, E_HALF, PACK], BF16, name="grouped2", align_bytes=64, bufs=6)
+            copy(
+                out=grouped2[q][:, first:last, :].rearrange("p (n i) t -> p n t i", i=RUN),
+                in_=raw2[g][:, :, half * E_HALF + first : half * E_HALF + last].rearrange("p t (n i) -> p n t i", i=RUN),
             )
-            nc.scalar.copy(
-                out=grouped[:, cut:E_HALF, :].rearrange("p (n i) t -> p n t i", i=RUN),
-                in_=raw2[g][:, :, half * E_HALF + cut : (half + 1) * E_HALF].rearrange("p t (n i) -> p n t i", i=RUN),
+
+        def regroup_w2_gpsimd(q, last, one):
+            half, g = divmod(q, PAIRS)
+            if q not in grouped2:
+                grouped2[q] = w2_pool.tile([P, E_HALF, PACK], BF16, name="grouped2", align_bytes=64, bufs=6)
+            nc.gpsimd.tensor_scalar(
+                out=grouped2[q][:, 0:last, :],
+                in0=raw2[g][:, :, half * E_HALF : half * E_HALF + last].rearrange("p t n -> p n t"),
+                scalar1=one,
+                scalar2=0.0,
+                op0=MULT,
+                op1=ADD,
             )
-            grouped2[q] = grouped
 
         def quantise_w2(q):
             codes = w2_pool.tile([P, E_HALF], U32, name="codes2", align_bytes=64)
@@ -332,34 +339,50 @@ def tile_fastfeedforwardnetwork_pa_kernel(tc, x, node_logits, node_b, w1, b1, w2
                     out=out_rows[b * P : (b + 1) * P, half * E_HALF : (half + 1) * E_HALF], in_=result[:]
                 )
 
+        regroup_w2(0, E_HALF // 2, E_HALF, nc.scalar.copy)
         for g in range(PAIRS):
-            first_matmul(g)
-            if g + 1 < PAIRS:
-                spread_probs(g + 1)
+            one = hidden_pool.tile([P, 1], F32, name="one")
+            nc.vector.memset(one[:], 1.0)
             bias_and_gate(g)
+            if g + 1 < PAIRS:
+                regroup_w2_gpsimd(g + 1, GPSIMD_CUT, one[:])
+                spread_probs(g + 1)
+            if g + 2 < PAIRS:
+                repeat_probs(g + 2)
+                load_w2(g + 2)
             if g + 1 < PAIRS:
                 quantise_w1(2 * g + 2)
                 quantise_w1(2 * g + 3)
-            else:
-                quantise_w2(0)
-                quantise_w2(1)
-            if g + 2 < PAIRS:
-                regroup_w1(2 * g + 4)
-                regroup_w1(2 * g + 5)
-            else:
-                regroup_w2(2 * (g + 2 - PAIRS))
-                regroup_w2(2 * (g + 2 - PAIRS) + 1)
-            relu_regroup(g)
+                first_matmul(g + 1)
             if g > 0:
-                quantise_h(g - 1)
-        quantise_h(PAIRS - 1)
+                second_matmul(g - 1)
+            else:
+                regroup_w2(0, 0, E_HALF // 2, nc.vector.tensor_copy)
+            relu_regroup(g)
+            for k in (2 * g + 4, 2 * g + 5):
+                if k < W1_PIECES:
+                    regroup_w1(k, 0, nc.scalar.copy)
+                    regroup_w1(k, 1, nc.scalar.copy)
+                    if k + 4 < W1_PIECES:
+                        load_w1(k + 4)
+            quantise_w2(g)
+            if g + 1 < PAIRS:
+                regroup_w2(g + 1, GPSIMD_CUT, E_HALF, nc.scalar.copy)
+            if g >= PAIRS - 2:
+                for q in (PAIRS + 2 * (g - PAIRS + 2), PAIRS + 2 * (g - PAIRS + 2) + 1):
+                    regroup_w2(q, 0, E_HALF, nc.scalar.copy)
+            quantise_h(g)
 
-        for q in range(PIECES):
+        ahead = 4
+        quantise_w2(PAIRS)
+        second_matmul(PAIRS - 1)
+        for q in range(PAIRS, PIECES):
+            if q + ahead < PIECES:
+                regroup_w2(q + ahead, 0, E_HALF // 2, nc.vector.tensor_copy)
+                regroup_w2(q + ahead, E_HALF // 2, E_HALF, nc.scalar.copy)
+            if q + 1 < PIECES:
+                quantise_w2(q + 1)
             second_matmul(q)
-            if q + 2 < PIECES:
-                quantise_w2(q + 2)
-            if q + 4 < PIECES:
-                regroup_w2(q + 4)
-            if q == PAIRS - 1 + STORE_LAG:
+            if q == PAIRS:
                 store_half(0)
         store_half(1)

@@ -10,6 +10,7 @@ U8 = mybir.dt.uint8
 FP8X4 = mybir.dt.float8_e4m3fn_x4
 ADD = mybir.AluOpType.add
 MULT = mybir.AluOpType.mult
+SUBTRACT = mybir.AluOpType.subtract
 RELU = mybir.ActivationFunctionType.Relu
 SIGMOID = mybir.ActivationFunctionType.Sigmoid
 
@@ -23,6 +24,7 @@ D_PASSES = D // K_PASS
 DEPTH = 4
 LEAVES = 2**DEPTH
 NODES = LEAVES - 1
+PARTS = 3
 F = 256
 PAIRS = LEAVES * F // K_PASS
 HALF_P = P // 2
@@ -32,7 +34,7 @@ PIECES = 2 * PAIRS
 RUN = 4
 PSUM_BANKS = 8
 W1_PIECES = PAIRS * D_PASSES
-GPSIMD_CUT = 320
+GPSIMD_CUT = 352
 RAW1_BUFS = 8
 
 FLOPS = 2 * TOKENS * D * LEAVES * F + 2 * TOKENS * LEAVES * F * E
@@ -56,7 +58,8 @@ def tile_fastfeedforwardnetwork_pa_kernel(tc, x, node_logits, node_b, w1, b1, w2
 
         identity = keep.tile([P, P], F32)
         bias = keep.tile([P, PAIRS * PACK], F32)
-        probs_by_token = keep.tile([P, TOKEN_BLOCKS, LEAVES], F32)
+        leaf_parts = keep.tile([P, TOKENS], BF16)
+        part_of_partition = keep.tile([P, LEAVES, HALF_P], BF16)
         probs = keep.tile([P, PAIRS, TOKENS], F32)
         x_codes = keep.tile([P, D_PASSES, TOKENS], U32, align_bytes=64)
         x_scales = keep.tile([P, D_PASSES, TOKENS], U8, align_bytes=64)
@@ -69,7 +72,6 @@ def tile_fastfeedforwardnetwork_pa_kernel(tc, x, node_logits, node_b, w1, b1, w2
         mx1 = {}
         grouped2 = {}
         mx2 = {}
-        repeated = {}
         pre_banks = {}
         gated = {}
         hidden = {}
@@ -129,23 +131,16 @@ def tile_fastfeedforwardnetwork_pa_kernel(tc, x, node_logits, node_b, w1, b1, w2
                 banks.append(bank)
             pre_banks[g] = banks
 
-        def repeat_probs(g):
-            rep = hidden_pool.tile([P, TOKEN_BLOCKS, P], F32, name="repeated")
-            nc.gpsimd.tensor_scalar(
-                out=rep[:].rearrange("p b (l i) -> p b l i", l=2),
-                in0=probs_by_token[:, :, 2 * g : 2 * g + 2].unsqueeze(3).to_broadcast([P, TOKEN_BLOCKS, 2, HALF_P]),
-                scalar1=1.0,
-                scalar2=0.0,
-                op0=MULT,
-                op1=ADD,
-            )
-            repeated[g] = rep
-
         def spread_probs(g):
-            bank = psum.tile([P, TOKEN_BLOCKS, P], F32, name="spread", tag="bank")
-            for b in range(TOKEN_BLOCKS):
-                nc.tensor.transpose(bank[:, b, :], repeated[g][:, b, :], identity[:])
-            nc.scalar.copy(out=probs[:, g, :], in_=bank[:].rearrange("p b n -> p (b n)"))
+            bank = psum.tile([P, TOKENS], F32, name="spread", tag="bank")
+            nc.tensor.matmul(
+                out=bank[:],
+                lhsT=part_of_partition[:, 2 * g : 2 * g + 2, :].rearrange("p l i -> p (l i)"),
+                rhs=leaf_parts[:],
+                start=True,
+                stop=True,
+            )
+            nc.scalar.copy(out=probs[:, g, :], in_=bank[:])
 
         def bias_and_gate(g):
             z = hidden_pool.tile([P, PACK, TOKENS], BF16, name="gated")
@@ -190,20 +185,32 @@ def tile_fastfeedforwardnetwork_pa_kernel(tc, x, node_logits, node_b, w1, b1, w2
             )
             nc.scalar.activation(out=warm[:], in_=warm[:], func=SIGMOID)
             make_identity(nc, identity[:])
+            identity_bf = setup.tile([P, P], BF16)
+            make_identity(nc, identity_bf[:])
+            parts = setup.tile([P, TOKEN_BLOCKS, P], BF16)
+            nc.gpsimd.memset(parts[:], 0.0)
+            leaf_of_row = setup.tile([P, 2, LEAVES], F32)
+            nc.gpsimd.tensor_tensor(out=leaf_of_row[:, 0, :], in0=identity[:, 0:LEAVES], in1=identity[:, LEAVES : 2 * LEAVES], op=ADD)
+            nc.gpsimd.tensor_tensor(out=leaf_of_row[:, 1, :], in0=leaf_of_row[:, 0, :], in1=identity[:, 2 * LEAVES : PARTS * LEAVES], op=ADD)
+            nc.gpsimd.tensor_scalar(
+                out=part_of_partition[:],
+                in0=leaf_of_row[:, 1, :].unsqueeze(2).to_broadcast([P, LEAVES, HALF_P]),
+                scalar1=1.0,
+                scalar2=0.0,
+                op0=MULT,
+                op1=ADD,
+            )
             load_w1(0)
             x_blocks = []
             for b in range(TOKEN_BLOCKS):
                 x_block = setup.tile([P, D], BF16, name="x%d" % b)
                 nc.sync.dma_start(out=x_block[:], in_=x_rows[b * P : (b + 1) * P, :])
                 x_blocks.append(x_block)
-            for k in (1, 2, 3):
+            for k in range(1, 6):
                 load_w1(k)
             load_w2(0)
-            load_w1(4)
-            load_w1(5)
-            load_w2(1)
-            load_w1(6)
-            load_w1(7)
+            for k in range(6, RAW1_BUFS):
+                load_w1(k)
 
             regroup_w1(0, 0, nc.vector.tensor_copy)
             regroup_w1(0, 1, nc.scalar.copy)
@@ -221,10 +228,7 @@ def tile_fastfeedforwardnetwork_pa_kernel(tc, x, node_logits, node_b, w1, b1, w2
 
             def tree_level(m, level):
                 nodes = 2**m
-                if m < DEPTH - 1:
-                    children = setup.tile([P, TOKEN_BLOCKS, 2 * nodes], F32, name="level%d" % m)[:]
-                else:
-                    children = probs_by_token[:]
+                children = setup.tile([P, TOKEN_BLOCKS, 2 * nodes], F32, name="level%d" % m)[:]
                 nc.vector.tensor_tensor(
                     out=children.rearrange("p b (n s) -> p b n s", s=2),
                     in0=level.unsqueeze(3).to_broadcast([P, TOKEN_BLOCKS, nodes, 2]),
@@ -250,27 +254,45 @@ def tile_fastfeedforwardnetwork_pa_kernel(tc, x, node_logits, node_b, w1, b1, w2
                     in_=x_turned[:].rearrange("p c u n -> p c n u"),
                 )
 
-            quantise_w1(0)
-            level = tree_level(1, gates[:, :, 0, :])
-            turn_x(0, nc.vector.tensor_copy)
-            level = tree_level(2, level)
-            turn_x(1, nc.scalar.copy)
-            turn_x(2, nc.vector.tensor_copy)
-            tree_level(3, level)
-            repeat_probs(0)
-            repeat_probs(1)
-            turn_x(3, nc.scalar.copy)
-            regroup_w1(1, 0, nc.vector.tensor_copy)
-            regroup_w1(1, 1, nc.scalar.copy)
-            for c in range(D_PASSES):
+            def round_part(s, rest):
+                nc.vector.tensor_copy(out=parts[:, :, s * LEAVES : (s + 1) * LEAVES], in_=rest)
+
+            def take_part(s, rest):
+                left = setup.tile([P, TOKEN_BLOCKS, LEAVES], F32, name="left%d" % s)[:]
+                nc.vector.tensor_tensor(out=left, in0=rest, in1=parts[:, :, s * LEAVES : (s + 1) * LEAVES], op=SUBTRACT)
+                return left
+
+            def quantise_x(c):
                 nc.vector.quantize_mx(
                     out=x_codes[:, c, :].bitcast(FP8X4),
                     scales=x_scales[:, c, :],
                     in_=x_grouped[:, c * TOKENS * PACK : (c + 1) * TOKENS * PACK],
                 )
-            spread_probs(0)
+
+            level = tree_level(1, gates[:, :, 0, :])
+            quantise_w1(0)
+            level = tree_level(2, level)
+            level = tree_level(3, level)
+            turn_x(0, nc.vector.tensor_copy)
+            round_part(0, level)
+            turn_x(1, nc.scalar.copy)
+            level = take_part(0, level)
+            turn_x(2, nc.vector.tensor_copy)
+            round_part(1, level)
+            turn_x(3, nc.scalar.copy)
+            level = take_part(1, level)
+            regroup_w1(1, 0, nc.vector.tensor_copy)
+            regroup_w1(1, 1, nc.scalar.copy)
+            round_part(2, level)
+            quantise_x(0)
+            quantise_x(1)
             quantise_w1(1)
+            parts_turned = psum.tile([P, TOKEN_BLOCKS, P], BF16, name="parts_turned", tag="bank")
+            for b in range(TOKEN_BLOCKS):
+                nc.tensor.transpose(parts_turned[:, b, :], parts[:, b, :], identity_bf[:])
+            nc.scalar.copy(out=leaf_parts[:], in_=parts_turned[:].rearrange("p b n -> p (b n)"))
             nc.vector.tensor_copy(out=bias[:], in_=b1_bf[:].rearrange("p g t -> p (g t)"))
+            spread_probs(0)
             first_matmul(0)
             for k in (2, 3):
                 regroup_w1(k, 0, nc.vector.tensor_copy)
@@ -281,21 +303,23 @@ def tile_fastfeedforwardnetwork_pa_kernel(tc, x, node_logits, node_b, w1, b1, w2
 
         def regroup_w2(q, first, last, copy):
             half, g = divmod(q, PAIRS)
-            if q not in grouped2:
+            if half == 1 and first == 0:
                 grouped2[q] = w2_pool.tile([P, E_HALF, PACK], BF16, name="grouped2", align_bytes=64, bufs=6)
             copy(
                 out=grouped2[q][:, first:last, :].rearrange("p (n i) t -> p n t i", i=RUN),
                 in_=raw2[g][:, :, half * E_HALF + first : half * E_HALF + last].rearrange("p t (n i) -> p n t i", i=RUN),
             )
 
-        def regroup_w2_gpsimd(q, last, one):
+        def release_gpsimd(q):
+            grouped2[q] = w2_pool.tile([P, E_HALF, PACK], BF16, name="grouped2", align_bytes=64, bufs=6)
+            nc.vector.memset(grouped2[q][:, 0, 0:1], 0.0)
+
+        def regroup_w2_gpsimd(q, last):
             half, g = divmod(q, PAIRS)
-            if q not in grouped2:
-                grouped2[q] = w2_pool.tile([P, E_HALF, PACK], BF16, name="grouped2", align_bytes=64, bufs=6)
             nc.gpsimd.tensor_scalar(
                 out=grouped2[q][:, 0:last, :],
                 in0=raw2[g][:, :, half * E_HALF : half * E_HALF + last].rearrange("p t n -> p n t"),
-                scalar1=one,
+                scalar1=1.0,
                 scalar2=0.0,
                 op0=MULT,
                 op1=ADD,
@@ -328,36 +352,29 @@ def tile_fastfeedforwardnetwork_pa_kernel(tc, x, node_logits, node_b, w1, b1, w2
                     stop=(g == PAIRS - 1),
                 )
 
-        def store_half(half):
+        def store_half(half, copies):
             for b in range(TOKEN_BLOCKS):
                 result = out_pool.tile([P, E_HALF], F32, name="result")
-                if b % 2 == 0:
-                    nc.vector.tensor_copy(out=result[:], in_=sums[(half, b)][:])
-                else:
-                    nc.scalar.copy(out=result[:], in_=sums[(half, b)][:])
+                copies[b % len(copies)](out=result[:], in_=sums[(half, b)][:])
                 nc.sync.dma_start(
                     out=out_rows[b * P : (b + 1) * P, half * E_HALF : (half + 1) * E_HALF], in_=result[:]
                 )
 
-        regroup_w2(0, E_HALF // 2, E_HALF, nc.scalar.copy)
         for g in range(PAIRS):
-            one = hidden_pool.tile([P, 1], F32, name="one")
-            nc.vector.memset(one[:], 1.0)
+            release_gpsimd(g)
             bias_and_gate(g)
+            regroup_w2_gpsimd(g, GPSIMD_CUT)
             if g + 1 < PAIRS:
-                regroup_w2_gpsimd(g + 1, GPSIMD_CUT, one[:])
                 spread_probs(g + 1)
-            if g + 2 < PAIRS:
-                repeat_probs(g + 2)
-                load_w2(g + 2)
-            if g + 1 < PAIRS:
+                load_w2(g + 1)
                 quantise_w1(2 * g + 2)
                 quantise_w1(2 * g + 3)
                 first_matmul(g + 1)
-            if g > 0:
-                second_matmul(g - 1)
             else:
-                regroup_w2(0, 0, E_HALF // 2, nc.vector.tensor_copy)
+                quantise_w2(g - 1)
+                quantise_w2(PAIRS)
+            if g >= 2:
+                second_matmul(g - 2)
             relu_regroup(g)
             for k in (2 * g + 4, 2 * g + 5):
                 if k < W1_PIECES:
@@ -365,24 +382,31 @@ def tile_fastfeedforwardnetwork_pa_kernel(tc, x, node_logits, node_b, w1, b1, w2
                     regroup_w1(k, 1, nc.scalar.copy)
                     if k + 4 < W1_PIECES:
                         load_w1(k + 4)
-            quantise_w2(g)
-            if g + 1 < PAIRS:
-                regroup_w2(g + 1, GPSIMD_CUT, E_HALF, nc.scalar.copy)
-            if g >= PAIRS - 2:
-                for q in (PAIRS + 2 * (g - PAIRS + 2), PAIRS + 2 * (g - PAIRS + 2) + 1):
-                    regroup_w2(q, 0, E_HALF, nc.scalar.copy)
+            regroup_w2(g, GPSIMD_CUT, E_HALF, nc.scalar.copy)
+            if 0 < g < PAIRS - 1:
+                quantise_w2(g - 1)
+            if g == PAIRS - 2:
+                regroup_w2(PAIRS, 0, E_HALF, nc.scalar.copy)
+                regroup_w2(PAIRS + 1, 0, E_HALF, nc.scalar.copy)
+            if g == PAIRS - 1:
+                quantise_w2(PAIRS + 1)
+                quantise_w2(PAIRS - 1)
+                for q in (PAIRS + 2, PAIRS + 3):
+                    regroup_w2(q, 0, E_HALF // 2, nc.vector.tensor_copy)
+                    regroup_w2(q, E_HALF // 2, E_HALF, nc.scalar.copy)
             quantise_h(g)
-
-        ahead = 4
-        quantise_w2(PAIRS)
+        second_matmul(PAIRS - 2)
+        second_matmul(PAIRS)
+        second_matmul(PAIRS + 1)
         second_matmul(PAIRS - 1)
-        for q in range(PAIRS, PIECES):
+
+        ahead = 2
+        for q in range(PAIRS + 2, PIECES):
             if q + ahead < PIECES:
                 regroup_w2(q + ahead, 0, E_HALF // 2, nc.vector.tensor_copy)
                 regroup_w2(q + ahead, E_HALF // 2, E_HALF, nc.scalar.copy)
-            if q + 1 < PIECES:
-                quantise_w2(q + 1)
+            quantise_w2(q)
+            if q == PAIRS + 2:
+                store_half(0, (nc.scalar.copy,))
             second_matmul(q)
-            if q == PAIRS:
-                store_half(0)
-        store_half(1)
+        store_half(1, (nc.vector.tensor_copy, nc.scalar.copy))

@@ -57,6 +57,7 @@ def tile_fastfeedforwardnetwork_pa_kernel(tc, x, node_logits, node_b, w1, b1, w2
         psum = stack.enter_context(tc.psum_pool(name="psum", bufs=PSUM_BANKS))
 
         identity = keep.tile([P, P], F32)
+        identity_bf = keep.tile([P, P], BF16)
         bias = keep.tile([P, PAIRS * PACK], F32)
         leaf_parts = keep.tile([P, TOKENS], BF16)
         part_of_partition = keep.tile([P, LEAVES, HALF_P], BF16)
@@ -100,6 +101,25 @@ def tile_fastfeedforwardnetwork_pa_kernel(tc, x, node_logits, node_b, w1, b1, w2
             copy(
                 out=grouped1[k][:, :, h * HALF_P : (h + 1) * HALF_P, :].rearrange("p t m j -> p m j t"),
                 in_=raw1[k][:, h, :, :].rearrange("p j (m t) -> p m j t", t=PACK),
+            )
+
+        def interleave_w1(k):
+            if k not in grouped1:
+                grouped1[k] = w1_pool.tile([P, PACK, P, PACK], BF16, name="grouped1", align_bytes=64)
+            bank = psum.tile([P, PACK, HALF_P, PACK], BF16, name="interleaved", tag="bank")
+            columns = raw1[k][:, 1, :, :].rearrange("p j (m t) -> p m j t", t=PACK)
+            for first in range(0, HALF_P, HALF_P // 2):
+                span = slice(first, first + HALF_P // 2)
+                nc.tensor.matmul(
+                    out=bank[:, :, span, :].rearrange("p t m j -> p m j t"),
+                    lhsT=identity_bf[:],
+                    rhs=columns[:, span, :, :],
+                    start=True,
+                    stop=True,
+                )
+            nc.scalar.copy(
+                out=grouped1[k][:, :, HALF_P:P, :].rearrange("p t m j -> p t (m j)"),
+                in_=bank[:].rearrange("p t m j -> p t (m j)"),
             )
 
         def quantise_w1(k):
@@ -185,7 +205,6 @@ def tile_fastfeedforwardnetwork_pa_kernel(tc, x, node_logits, node_b, w1, b1, w2
             )
             nc.scalar.activation(out=warm[:], in_=warm[:], func=SIGMOID)
             make_identity(nc, identity[:])
-            identity_bf = setup.tile([P, P], BF16)
             make_identity(nc, identity_bf[:])
             parts = setup.tile([P, TOKEN_BLOCKS, P], BF16)
             nc.gpsimd.memset(parts[:], 0.0)
@@ -296,7 +315,7 @@ def tile_fastfeedforwardnetwork_pa_kernel(tc, x, node_logits, node_b, w1, b1, w2
             first_matmul(0)
             for k in (2, 3):
                 regroup_w1(k, 0, nc.vector.tensor_copy)
-                regroup_w1(k, 1, nc.scalar.copy)
+                interleave_w1(k)
 
         w2_pool = stack.enter_context(tc.tile_pool(name="w2", bufs=4))
         out_pool = stack.enter_context(tc.tile_pool(name="out", bufs=TOKEN_BLOCKS))
@@ -367,6 +386,8 @@ def tile_fastfeedforwardnetwork_pa_kernel(tc, x, node_logits, node_b, w1, b1, w2
             if g + 1 < PAIRS:
                 spread_probs(g + 1)
                 load_w2(g + 1)
+                if 2 * g + 4 < W1_PIECES:
+                    interleave_w1(2 * g + 4)
                 quantise_w1(2 * g + 2)
                 quantise_w1(2 * g + 3)
                 first_matmul(g + 1)
@@ -379,7 +400,8 @@ def tile_fastfeedforwardnetwork_pa_kernel(tc, x, node_logits, node_b, w1, b1, w2
             for k in (2 * g + 4, 2 * g + 5):
                 if k < W1_PIECES:
                     regroup_w1(k, 0, nc.scalar.copy)
-                    regroup_w1(k, 1, nc.scalar.copy)
+                    if k % 2 == 1:
+                        regroup_w1(k, 1, nc.scalar.copy)
                     if k + 4 < W1_PIECES:
                         load_w1(k + 4)
             regroup_w2(g, GPSIMD_CUT, E_HALF, nc.scalar.copy)

@@ -162,6 +162,12 @@ def tile_fastfeedforwardnetwork_pa_kernel(tc, x, node_logits, node_b, w1, b1, w2
             )
             nc.scalar.copy(out=probs[:, g, :], in_=bank[:])
 
+        def spread_first_probs():
+            bank = psum.tile([P, TOKEN_BLOCKS, P], F32, name="spread", tag="bank")
+            for b in range(TOKEN_BLOCKS):
+                nc.tensor.transpose(bank[:, b, :], repeated[:, b, :], identity[:])
+            nc.scalar.copy(out=probs[:, 0, :], in_=bank[:].rearrange("p b n -> p (b n)"))
+
         def bias_and_gate(g):
             z = hidden_pool.tile([P, PACK, TOKENS], BF16, name="gated")
             for t in range(PACK):
@@ -194,6 +200,14 @@ def tile_fastfeedforwardnetwork_pa_kernel(tc, x, node_logits, node_b, w1, b1, w2
         with tc.tile_pool(name="setup", bufs=1) as setup:
             warm = setup.tile([P, 1], F32)
             nc.vector.memset(warm[:], 0.0)
+            zeros = setup.tile([P, TOKENS], BF16)
+            nc.vector.memset(zeros[:], 0.0)
+
+            def keep_busy(times):
+                idle = psum.tile([P, TOKENS], F32, name="idle", tag="bank")
+                for i in range(times):
+                    nc.tensor.matmul(out=idle[:], lhsT=zeros[:, 0:P], rhs=zeros[:], start=True, stop=True)
+
             logits = setup.tile([P, TOKEN_BLOCKS, NODES], BF16)
             nc.scalar.dma_start(out=logits[:], in_=logit_rows.rearrange("(b p) n -> p b n", p=P))
             node_bias = setup.tile([P, NODES], BF16)
@@ -248,7 +262,7 @@ def tile_fastfeedforwardnetwork_pa_kernel(tc, x, node_logits, node_b, w1, b1, w2
             def tree_level(m, level):
                 nodes = 2**m
                 children = setup.tile([P, TOKEN_BLOCKS, 2 * nodes], F32, name="level%d" % m)[:]
-                nc.vector.tensor_tensor(
+                nc.gpsimd.tensor_tensor(
                     out=children.rearrange("p b (n s) -> p b n s", s=2),
                     in0=level.unsqueeze(3).to_broadcast([P, TOKEN_BLOCKS, nodes, 2]),
                     in1=gates[:, :, nodes - 1 : 2 * nodes - 1, :],
@@ -281,41 +295,53 @@ def tile_fastfeedforwardnetwork_pa_kernel(tc, x, node_logits, node_b, w1, b1, w2
                 nc.vector.tensor_tensor(out=left, in0=rest, in1=parts[:, :, s * LEAVES : (s + 1) * LEAVES], op=SUBTRACT)
                 return left
 
-            def quantise_x(c):
-                nc.vector.quantize_mx(
-                    out=x_codes[:, c, :].bitcast(FP8X4),
-                    scales=x_scales[:, c, :],
-                    in_=x_grouped[:, c * TOKENS * PACK : (c + 1) * TOKENS * PACK],
-                )
+            def quantise_x(first, last):
+                for c in range(D_PASSES):
+                    nc.vector.quantize_mx(
+                        out=x_codes[:, c, first:last].bitcast(FP8X4),
+                        scales=x_scales[:, c, first:last],
+                        in_=x_grouped[:, (c * TOKENS + first) * PACK : (c * TOKENS + last) * PACK],
+                    )
 
-            level = tree_level(1, gates[:, :, 0, :])
+            level = gates[:, :, 0, :]
+            for m in range(1, DEPTH):
+                level = tree_level(m, level)
             quantise_w1(0)
-            level = tree_level(2, level)
-            level = tree_level(3, level)
+            keep_busy(4)
             turn_x(0, nc.vector.tensor_copy)
-            round_part(0, level)
+            keep_busy(1)
             turn_x(1, nc.scalar.copy)
-            level = take_part(0, level)
+            keep_busy(1)
+            repeated = setup.tile([P, TOKEN_BLOCKS, P], F32)
+            nc.vector.tensor_copy(
+                out=repeated[:].rearrange("p b (l i) -> p b l i", l=2),
+                in_=level[:, :, 0:2].unsqueeze(3).to_broadcast([P, TOKEN_BLOCKS, 2, HALF_P]),
+            )
             turn_x(2, nc.vector.tensor_copy)
-            round_part(1, level)
+            quantise_x(0, TOKENS // 2)
+            keep_busy(1)
             turn_x(3, nc.scalar.copy)
-            level = take_part(1, level)
+            keep_busy(2)
             regroup_w1(1, 0, nc.vector.tensor_copy)
             regroup_w1(1, 1, nc.scalar.copy)
-            round_part(2, level)
-            quantise_x(0)
-            quantise_x(1)
+            quantise_x(TOKENS // 2, TOKENS)
             quantise_w1(1)
+            spread_first_probs()
+            first_matmul(0)
+            nc.vector.tensor_copy(out=bias[:], in_=b1_bf[:].rearrange("p g t -> p (g t)"))
+            round_part(0, level)
+            regroup_w1(2, 1, nc.scalar.copy)
+            regroup_w1(2, 0, nc.vector.tensor_copy)
+            level = take_part(0, level)
+            regroup_w1(3, 1, nc.scalar.copy)
+            regroup_w1(3, 0, nc.vector.tensor_copy)
+            round_part(1, level)
+            level = take_part(1, level)
+            round_part(2, level)
             parts_turned = psum.tile([P, TOKEN_BLOCKS, P], BF16, name="parts_turned", tag="bank")
             for b in range(TOKEN_BLOCKS):
                 nc.tensor.transpose(parts_turned[:, b, :], parts[:, b, :], identity_bf[:])
             nc.scalar.copy(out=leaf_parts[:], in_=parts_turned[:].rearrange("p b n -> p (b n)"))
-            nc.vector.tensor_copy(out=bias[:], in_=b1_bf[:].rearrange("p g t -> p (g t)"))
-            spread_probs(0)
-            first_matmul(0)
-            for k in (2, 3):
-                regroup_w1(k, 0, nc.vector.tensor_copy)
-                interleave_w1(k)
 
         w2_pool = stack.enter_context(tc.tile_pool(name="w2", bufs=4))
         out_pool = stack.enter_context(tc.tile_pool(name="out", bufs=TOKEN_BLOCKS))
@@ -371,13 +397,10 @@ def tile_fastfeedforwardnetwork_pa_kernel(tc, x, node_logits, node_b, w1, b1, w2
                     stop=(g == PAIRS - 1),
                 )
 
-        def store_half(half, copies):
-            for b in range(TOKEN_BLOCKS):
-                result = out_pool.tile([P, E_HALF], F32, name="result")
-                copies[b % len(copies)](out=result[:], in_=sums[(half, b)][:])
-                nc.sync.dma_start(
-                    out=out_rows[b * P : (b + 1) * P, half * E_HALF : (half + 1) * E_HALF], in_=result[:]
-                )
+        def store(half, b, copy):
+            result = out_pool.tile([P, E_HALF], F32, name="result")
+            copy(out=result[:], in_=sums[(half, b)][:])
+            nc.sync.dma_start(out=out_rows[b * P : (b + 1) * P, half * E_HALF : (half + 1) * E_HALF], in_=result[:])
 
         for g in range(PAIRS):
             release_gpsimd(g)
@@ -413,22 +436,21 @@ def tile_fastfeedforwardnetwork_pa_kernel(tc, x, node_logits, node_b, w1, b1, w2
             if g == PAIRS - 1:
                 quantise_w2(PAIRS + 1)
                 quantise_w2(PAIRS - 1)
-                for q in (PAIRS + 2, PAIRS + 3):
-                    regroup_w2(q, 0, E_HALF // 2, nc.vector.tensor_copy)
-                    regroup_w2(q, E_HALF // 2, E_HALF, nc.scalar.copy)
             quantise_h(g)
+        regroup_w2(PAIRS + 2, 0, E_HALF // 2, nc.vector.tensor_copy)
+        regroup_w2(PAIRS + 2, E_HALF // 2, E_HALF, nc.scalar.copy)
         second_matmul(PAIRS - 2)
         second_matmul(PAIRS)
         second_matmul(PAIRS + 1)
         second_matmul(PAIRS - 1)
 
-        ahead = 2
         for q in range(PAIRS + 2, PIECES):
-            if q + ahead < PIECES:
-                regroup_w2(q + ahead, 0, E_HALF // 2, nc.vector.tensor_copy)
-                regroup_w2(q + ahead, E_HALF // 2, E_HALF, nc.scalar.copy)
+            if q + 1 < PIECES:
+                regroup_w2(q + 1, 0, E_HALF // 2, nc.vector.tensor_copy)
+                regroup_w2(q + 1, E_HALF // 2, E_HALF, nc.scalar.copy)
             quantise_w2(q)
-            if q == PAIRS + 2:
-                store_half(0, (nc.scalar.copy,))
             second_matmul(q)
-        store_half(1, (nc.vector.tensor_copy, nc.scalar.copy))
+            if q >= PIECES - TOKEN_BLOCKS:
+                store(0, q - PIECES + TOKEN_BLOCKS, nc.scalar.copy)
+        for b in range(TOKEN_BLOCKS):
+            store(1, b, (nc.vector.tensor_copy, nc.scalar.copy)[b % 2])

@@ -220,7 +220,7 @@ def tile_fastfeedforwardnetwork_pa_kernel(tc, x, node_logits, node_b, w1, b1, w2
             nc.scalar.activation(out=warm[:], in_=warm[:], func=SIGMOID)
             make_identity(nc, identity[:])
             make_identity(nc, identity_bf[:])
-            parts = setup.tile([P, TOKEN_BLOCKS, P], BF16)
+            parts = keep.tile([P, TOKEN_BLOCKS, P], BF16)
             nc.gpsimd.memset(parts[:], 0.0)
             leaf_of_row = setup.tile([P, 2, LEAVES], F32)
             nc.gpsimd.tensor_tensor(out=leaf_of_row[:, 0, :], in0=identity[:, 0:LEAVES], in1=identity[:, LEAVES : 2 * LEAVES], op=ADD)
@@ -239,10 +239,10 @@ def tile_fastfeedforwardnetwork_pa_kernel(tc, x, node_logits, node_b, w1, b1, w2
                 x_block = setup.tile([P, D], BF16, name="x%d" % b)
                 nc.sync.dma_start(out=x_block[:], in_=x_rows[b * P : (b + 1) * P, :])
                 x_blocks.append(x_block)
-            for k in range(1, 6):
+            for k in range(1, 4):
                 load_w1(k)
             load_w2(0)
-            for k in range(6, RAW1_BUFS):
+            for k in range(4, RAW1_BUFS):
                 load_w1(k)
 
             regroup_w1(0, 0, nc.vector.tensor_copy)
@@ -261,7 +261,7 @@ def tile_fastfeedforwardnetwork_pa_kernel(tc, x, node_logits, node_b, w1, b1, w2
 
             def tree_level(m, level):
                 nodes = 2**m
-                children = setup.tile([P, TOKEN_BLOCKS, 2 * nodes], F32, name="level%d" % m)[:]
+                children = keep.tile([P, TOKEN_BLOCKS, 2 * nodes], F32, name="level%d" % m)[:]
                 nc.gpsimd.tensor_tensor(
                     out=children.rearrange("p b (n s) -> p b n s", s=2),
                     in0=level.unsqueeze(3).to_broadcast([P, TOKEN_BLOCKS, nodes, 2]),
@@ -270,8 +270,7 @@ def tile_fastfeedforwardnetwork_pa_kernel(tc, x, node_logits, node_b, w1, b1, w2
                 )
                 return children
 
-            x_grouped = setup.tile([P, D_PASSES * TOKENS * PACK], BF16, align_bytes=64)
-            x_grouped_words = x_grouped[:].bitcast(F32).rearrange("p (c n u) -> p c n u", c=D_PASSES, u=2)
+            x_grouped = {}
 
             def turn_x(b, copy):
                 words = x_blocks[b][:].bitcast(F32)
@@ -282,25 +281,27 @@ def tile_fastfeedforwardnetwork_pa_kernel(tc, x, node_logits, node_b, w1, b1, w2
                         nc.tensor.transpose(
                             x_turned[:, c, u, :], words[:, first : (c + 1) * (K_PASS // 2) : 2], identity[:]
                         )
+                grouped = setup.tile([P, D_PASSES, P * PACK], BF16, name="x_grouped%d" % b, align_bytes=64)
                 copy(
-                    out=x_grouped_words[:, :, b * P : (b + 1) * P, :],
+                    out=grouped[:].bitcast(F32).rearrange("p c (n u) -> p c n u", u=2),
                     in_=x_turned[:].rearrange("p c u n -> p c n u"),
                 )
+                x_grouped[b] = grouped
 
             def round_part(s, rest):
                 nc.vector.tensor_copy(out=parts[:, :, s * LEAVES : (s + 1) * LEAVES], in_=rest)
 
             def take_part(s, rest):
-                left = setup.tile([P, TOKEN_BLOCKS, LEAVES], F32, name="left%d" % s)[:]
+                left = keep.tile([P, TOKEN_BLOCKS, LEAVES], F32, name="left%d" % s)[:]
                 nc.vector.tensor_tensor(out=left, in0=rest, in1=parts[:, :, s * LEAVES : (s + 1) * LEAVES], op=SUBTRACT)
                 return left
 
-            def quantise_x(first, last):
+            def quantise_x(b):
                 for c in range(D_PASSES):
                     nc.vector.quantize_mx(
-                        out=x_codes[:, c, first:last].bitcast(FP8X4),
-                        scales=x_scales[:, c, first:last],
-                        in_=x_grouped[:, (c * TOKENS + first) * PACK : (c * TOKENS + last) * PACK],
+                        out=x_codes[:, c, b * P : (b + 1) * P].bitcast(FP8X4),
+                        scales=x_scales[:, c, b * P : (b + 1) * P],
+                        in_=x_grouped[b][:, c, :],
                     )
 
             level = gates[:, :, 0, :]
@@ -312,19 +313,21 @@ def tile_fastfeedforwardnetwork_pa_kernel(tc, x, node_logits, node_b, w1, b1, w2
             keep_busy(1)
             turn_x(1, nc.scalar.copy)
             keep_busy(1)
-            repeated = setup.tile([P, TOKEN_BLOCKS, P], F32)
+            repeated = keep.tile([P, TOKEN_BLOCKS, P], F32)
             nc.vector.tensor_copy(
                 out=repeated[:].rearrange("p b (l i) -> p b l i", l=2),
                 in_=level[:, :, 0:2].unsqueeze(3).to_broadcast([P, TOKEN_BLOCKS, 2, HALF_P]),
             )
+            quantise_x(0)
             turn_x(2, nc.vector.tensor_copy)
-            quantise_x(0, TOKENS // 2)
+            quantise_x(1)
             keep_busy(1)
             turn_x(3, nc.scalar.copy)
             keep_busy(2)
+            quantise_x(2)
             regroup_w1(1, 0, nc.vector.tensor_copy)
             regroup_w1(1, 1, nc.scalar.copy)
-            quantise_x(TOKENS // 2, TOKENS)
+            quantise_x(3)
             quantise_w1(1)
             spread_first_probs()
             first_matmul(0)

@@ -34,7 +34,8 @@ PIECES = 2 * PAIRS
 RUN = 4
 PSUM_BANKS = 8
 W1_PIECES = PAIRS * D_PASSES
-GPSIMD_CUT = 352
+RELU_CUT = 448
+GPSIMD_CUT = 304
 RAW1_BUFS = 8
 
 FLOPS = 2 * TOKENS * D * LEAVES * F + 2 * TOKENS * LEAVES * F * E
@@ -51,7 +52,7 @@ def tile_fastfeedforwardnetwork_pa_kernel(tc, x, node_logits, node_b, w1, b1, w2
         stack.enter_context(tc.manual_schedule())
         keep = stack.enter_context(tc.tile_pool(name="keep", bufs=1))
         raw1_pool = stack.enter_context(tc.tile_pool(name="raw1", bufs=RAW1_BUFS))
-        raw2_pool = stack.enter_context(tc.tile_pool(name="raw2", bufs=PAIRS))
+        raw2_pool = stack.enter_context(tc.tile_pool(name="raw2", bufs=PIECES))
         w1_pool = stack.enter_context(tc.tile_pool(name="w1", bufs=4))
         hidden_pool = stack.enter_context(tc.tile_pool(name="hidden", bufs=2))
         psum = stack.enter_context(tc.psum_pool(name="psum", bufs=PSUM_BANKS))
@@ -87,13 +88,16 @@ def tile_fastfeedforwardnetwork_pa_kernel(tc, x, node_logits, node_b, w1, b1, w2
             )
             raw1[k] = raw
 
-        def load_w2(g):
-            raw = raw2_pool.tile([P, PACK, E], BF16, name="raw2")
+        def load_w2(q):
+            half, g = divmod(q, PAIRS)
+            raw = raw2_pool.tile([P, PACK, E_HALF], BF16, name="raw2")
             nc.sync.dma_start(
-                out=raw[:].rearrange("p t e -> p (t e)"),
-                in_=w2_rows[g * K_PASS : (g + 1) * K_PASS, :].rearrange("(p t) e -> p (t e)", t=PACK),
+                out=raw[:],
+                in_=w2_rows[g * K_PASS : (g + 1) * K_PASS, half * E_HALF : (half + 1) * E_HALF].rearrange(
+                    "(p t) e -> p t e", t=PACK
+                ),
             )
-            raw2[g] = raw
+            raw2[q] = raw
 
         def regroup_w1(k, h, copy):
             if k not in grouped1:
@@ -184,9 +188,14 @@ def tile_fastfeedforwardnetwork_pa_kernel(tc, x, node_logits, node_b, w1, b1, w2
         def relu_regroup(g):
             h = hidden_pool.tile([P, TOKENS, PACK], BF16, name="hidden", align_bytes=64)
             nc.vector.tensor_scalar_max(
-                out=h[:].rearrange("p (n i) t -> p n t i", i=RUN),
-                in0=gated[g][:].rearrange("p t (n i) -> p n t i", i=RUN),
+                out=h[:, 0:RELU_CUT, :].rearrange("p (n i) t -> p n t i", i=RUN),
+                in0=gated[g][:, :, 0:RELU_CUT].rearrange("p t (n i) -> p n t i", i=RUN),
                 scalar1=0.0,
+            )
+            nc.scalar.activation(
+                out=h[:, RELU_CUT:TOKENS, :].rearrange("p (n i) t -> p n t i", i=RUN),
+                in_=gated[g][:, :, RELU_CUT:TOKENS].rearrange("p t (n i) -> p n t i", i=RUN),
+                func=RELU,
             )
             hidden[g] = h
 
@@ -350,12 +359,11 @@ def tile_fastfeedforwardnetwork_pa_kernel(tc, x, node_logits, node_b, w1, b1, w2
         out_pool = stack.enter_context(tc.tile_pool(name="out", bufs=TOKEN_BLOCKS))
 
         def regroup_w2(q, first, last, copy):
-            half, g = divmod(q, PAIRS)
-            if half == 1 and first == 0:
+            if q >= PAIRS and first == 0:
                 grouped2[q] = w2_pool.tile([P, E_HALF, PACK], BF16, name="grouped2", align_bytes=64, bufs=6)
             copy(
                 out=grouped2[q][:, first:last, :].rearrange("p (n i) t -> p n t i", i=RUN),
-                in_=raw2[g][:, :, half * E_HALF + first : half * E_HALF + last].rearrange("p t (n i) -> p n t i", i=RUN),
+                in_=raw2[q][:, :, first:last].rearrange("p t (n i) -> p n t i", i=RUN),
             )
 
         def release_gpsimd(q):
@@ -363,10 +371,9 @@ def tile_fastfeedforwardnetwork_pa_kernel(tc, x, node_logits, node_b, w1, b1, w2
             nc.vector.memset(grouped2[q][:, 0, 0:1], 0.0)
 
         def regroup_w2_gpsimd(q, last):
-            half, g = divmod(q, PAIRS)
             nc.gpsimd.tensor_scalar(
                 out=grouped2[q][:, 0:last, :],
-                in0=raw2[g][:, :, half * E_HALF : half * E_HALF + last].rearrange("p t n -> p n t"),
+                in0=raw2[q][:, :, 0:last].rearrange("p t n -> p n t"),
                 scalar1=1.0,
                 scalar2=0.0,
                 op0=MULT,
@@ -430,6 +437,9 @@ def tile_fastfeedforwardnetwork_pa_kernel(tc, x, node_logits, node_b, w1, b1, w2
                         regroup_w1(k, 1, nc.scalar.copy)
                     if k + 4 < W1_PIECES:
                         load_w1(k + 4)
+            if PAIRS - 5 <= g < PAIRS - 1:
+                load_w2(2 * g + 2)
+                load_w2(2 * g + 3)
             regroup_w2(g, GPSIMD_CUT, E_HALF, nc.scalar.copy)
             if 0 < g < PAIRS - 1:
                 quantise_w2(g - 1)

@@ -34,7 +34,8 @@ PIECES = 2 * PAIRS
 RUN = 4
 PSUM_BANKS = 8
 W1_PIECES = PAIRS * D_PASSES
-RELU_CUT = 448
+RELU_CUT = 416
+LAST_CUT = 272
 GPSIMD_CUT = 304
 RAW1_BUFS = 8
 
@@ -99,20 +100,20 @@ def tile_fastfeedforwardnetwork_pa_kernel(tc, x, node_logits, node_b, w1, b1, w2
             )
             raw2[q] = raw
 
-        def regroup_w1(k, h, copy):
+        def regroup_w1(k, h, copy, skip=0):
             if k not in grouped1:
                 grouped1[k] = w1_pool.tile([P, PACK, P, PACK], BF16, name="grouped1", align_bytes=64)
             copy(
-                out=grouped1[k][:, :, h * HALF_P : (h + 1) * HALF_P, :].rearrange("p t m j -> p m j t"),
-                in_=raw1[k][:, h, :, :].rearrange("p j (m t) -> p m j t", t=PACK),
+                out=grouped1[k][:, :, h * HALF_P + skip : (h + 1) * HALF_P, :].rearrange("p t m j -> p m j t"),
+                in_=raw1[k][:, h, :, skip * PACK : F].rearrange("p j (m t) -> p m j t", t=PACK),
             )
 
-        def interleave_w1(k):
+        def interleave_w1(k, columns_m):
             if k not in grouped1:
                 grouped1[k] = w1_pool.tile([P, PACK, P, PACK], BF16, name="grouped1", align_bytes=64)
-            bank = psum.tile([P, PACK, HALF_P, PACK], BF16, name="interleaved", tag="bank")
+            bank = psum.tile([P, PACK, columns_m, PACK], BF16, name="interleaved", tag="bank")
             columns = raw1[k][:, 1, :, :].rearrange("p j (m t) -> p m j t", t=PACK)
-            for first in range(0, HALF_P, HALF_P // 2):
+            for first in range(0, columns_m, HALF_P // 2):
                 span = slice(first, first + HALF_P // 2)
                 nc.tensor.matmul(
                     out=bank[:, :, span, :].rearrange("p t m j -> p m j t"),
@@ -122,7 +123,7 @@ def tile_fastfeedforwardnetwork_pa_kernel(tc, x, node_logits, node_b, w1, b1, w2
                     stop=True,
                 )
             nc.scalar.copy(
-                out=grouped1[k][:, :, HALF_P:P, :].rearrange("p t m j -> p t (m j)"),
+                out=grouped1[k][:, :, HALF_P : HALF_P + columns_m, :].rearrange("p t m j -> p t (m j)"),
                 in_=bank[:].rearrange("p t m j -> p t (m j)"),
             )
 
@@ -187,16 +188,18 @@ def tile_fastfeedforwardnetwork_pa_kernel(tc, x, node_logits, node_b, w1, b1, w2
 
         def relu_regroup(g):
             h = hidden_pool.tile([P, TOKENS, PACK], BF16, name="hidden", align_bytes=64)
+            cut = RELU_CUT if g > 0 else TOKENS
             nc.vector.tensor_scalar_max(
-                out=h[:, 0:RELU_CUT, :].rearrange("p (n i) t -> p n t i", i=RUN),
-                in0=gated[g][:, :, 0:RELU_CUT].rearrange("p t (n i) -> p n t i", i=RUN),
+                out=h[:, 0:cut, :].rearrange("p (n i) t -> p n t i", i=RUN),
+                in0=gated[g][:, :, 0:cut].rearrange("p t (n i) -> p n t i", i=RUN),
                 scalar1=0.0,
             )
-            nc.scalar.activation(
-                out=h[:, RELU_CUT:TOKENS, :].rearrange("p (n i) t -> p n t i", i=RUN),
-                in_=gated[g][:, :, RELU_CUT:TOKENS].rearrange("p t (n i) -> p n t i", i=RUN),
-                func=RELU,
-            )
+            if cut < TOKENS:
+                nc.scalar.activation(
+                    out=h[:, cut:TOKENS, :].rearrange("p (n i) t -> p n t i", i=RUN),
+                    in_=gated[g][:, :, cut:TOKENS].rearrange("p t (n i) -> p n t i", i=RUN),
+                    func=RELU,
+                )
             hidden[g] = h
 
         def quantise_h(g):
@@ -350,6 +353,7 @@ def tile_fastfeedforwardnetwork_pa_kernel(tc, x, node_logits, node_b, w1, b1, w2
             round_part(1, level)
             level = take_part(1, level)
             round_part(2, level)
+            regroup_w1(4, 0, nc.scalar.copy)
             parts_turned = psum.tile([P, TOKEN_BLOCKS, P], BF16, name="parts_turned", tag="bank")
             for b in range(TOKEN_BLOCKS):
                 nc.tensor.transpose(parts_turned[:, b, :], parts[:, b, :], identity_bf[:])
@@ -420,7 +424,8 @@ def tile_fastfeedforwardnetwork_pa_kernel(tc, x, node_logits, node_b, w1, b1, w2
                 spread_probs(g + 1)
                 load_w2(g + 1)
                 if 2 * g + 4 < W1_PIECES:
-                    interleave_w1(2 * g + 4)
+                    interleave_w1(2 * g + 4, HALF_P)
+                    interleave_w1(2 * g + 5, HALF_P // 2)
                 quantise_w1(2 * g + 2)
                 quantise_w1(2 * g + 3)
                 first_matmul(g + 1)
@@ -432,9 +437,10 @@ def tile_fastfeedforwardnetwork_pa_kernel(tc, x, node_logits, node_b, w1, b1, w2
             relu_regroup(g)
             for k in (2 * g + 4, 2 * g + 5):
                 if k < W1_PIECES:
-                    regroup_w1(k, 0, nc.scalar.copy)
+                    if k > 4:
+                        regroup_w1(k, 0, nc.scalar.copy)
                     if k % 2 == 1:
-                        regroup_w1(k, 1, nc.scalar.copy)
+                        regroup_w1(k, 1, nc.scalar.copy, HALF_P // 2)
                     if k + 4 < W1_PIECES:
                         load_w1(k + 4)
             if PAIRS - 5 <= g < PAIRS - 1:
@@ -459,8 +465,8 @@ def tile_fastfeedforwardnetwork_pa_kernel(tc, x, node_logits, node_b, w1, b1, w2
 
         for q in range(PAIRS + 2, PIECES):
             if q + 1 < PIECES:
-                regroup_w2(q + 1, 0, E_HALF // 2, nc.vector.tensor_copy)
-                regroup_w2(q + 1, E_HALF // 2, E_HALF, nc.scalar.copy)
+                regroup_w2(q + 1, 0, LAST_CUT, nc.vector.tensor_copy)
+                regroup_w2(q + 1, LAST_CUT, E_HALF, nc.scalar.copy)
             quantise_w2(q)
             second_matmul(q)
             if q >= PIECES - TOKEN_BLOCKS:

from contextlib import ExitStack

import concourse.mybir as mybir
from concourse.masks import make_identity

F32 = mybir.dt.float32
BF16 = mybir.dt.bfloat16
U32 = mybir.dt.uint32
U8 = mybir.dt.uint8
FP8X4 = mybir.dt.float8_e4m3fn_x4
ADD = mybir.AluOpType.add
MULT = mybir.AluOpType.mult
SUBTRACT = mybir.AluOpType.subtract
RELU = mybir.ActivationFunctionType.Relu
SIGMOID = mybir.ActivationFunctionType.Sigmoid

P = 128
PACK = 4
K_PASS = P * PACK
TOKENS = 512
TOKEN_BLOCKS = TOKENS // P
D = 1024
D_PASSES = D // K_PASS
DEPTH = 4
LEAVES = 2**DEPTH
NODES = LEAVES - 1
PARTS = 3
F = 256
PAIRS = LEAVES * F // K_PASS
HALF_P = P // 2
E = 1024
E_HALF = 512
PIECES = 2 * PAIRS
RUN = 4
PSUM_BANKS = 8
W1_PIECES = PAIRS * D_PASSES
RELU_CUT = 416
LAST_CUT = 272
GPSIMD_CUT = 304
RAW1_BUFS = 8

FLOPS = 2 * TOKENS * D * LEAVES * F + 2 * TOKENS * LEAVES * F * E


def tile_fastfeedforwardnetwork_pa_kernel(tc, x, node_logits, node_b, w1, b1, w2, out):
    nc = tc.nc
    x_rows = x.flatten_outer_dims()
    logit_rows = node_logits.flatten_outer_dims()
    w2_rows = w2.flatten_outer_dims()
    out_rows = out.flatten_outer_dims()

    with ExitStack() as stack:
        stack.enter_context(tc.manual_schedule())
        keep = stack.enter_context(tc.tile_pool(name="keep", bufs=1))
        raw1_pool = stack.enter_context(tc.tile_pool(name="raw1", bufs=RAW1_BUFS))
        raw2_pool = stack.enter_context(tc.tile_pool(name="raw2", bufs=PIECES))
        w1_pool = stack.enter_context(tc.tile_pool(name="w1", bufs=4))
        hidden_pool = stack.enter_context(tc.tile_pool(name="hidden", bufs=2))
        psum = stack.enter_context(tc.psum_pool(name="psum", bufs=PSUM_BANKS))

        identity = keep.tile([P, P], F32)
        identity_bf = keep.tile([P, P], BF16)
        bias = keep.tile([P, PAIRS * PACK], F32)
        leaf_parts = keep.tile([P, TOKENS], BF16)
        part_of_partition = keep.tile([P, LEAVES, HALF_P], BF16)
        probs = keep.tile([P, PAIRS, TOKENS], F32)
        x_codes = keep.tile([P, D_PASSES, TOKENS], U32, align_bytes=64)
        x_scales = keep.tile([P, D_PASSES, TOKENS], U8, align_bytes=64)
        h_codes = keep.tile([P, PAIRS, TOKENS], U32, align_bytes=64)
        h_scales = keep.tile([P, PAIRS, TOKENS], U8, align_bytes=64)

        raw1 = {}
        raw2 = {}
        grouped1 = {}
        mx1 = {}
        grouped2 = {}
        mx2 = {}
        pre_banks = {}
        gated = {}
        hidden = {}
        sums = {}

        def load_w1(k):
            g, c = divmod(k, D_PASSES)
            raw = raw1_pool.tile([P, 2, PACK, F], BF16, name="raw1")
            nc.sync.dma_start(
                out=raw[:].rearrange("p h j f -> p h (j f)"),
                in_=w1[2 * g : 2 * g + 2, c * K_PASS : (c + 1) * K_PASS, :].rearrange("h (p j) f -> p h (j f)", j=PACK),
            )
            raw1[k] = raw

        def load_w2(q):
            half, g = divmod(q, PAIRS)
            raw = raw2_pool.tile([P, PACK, E_HALF], BF16, name="raw2")
            nc.sync.dma_start(
                out=raw[:],
                in_=w2_rows[g * K_PASS : (g + 1) * K_PASS, half * E_HALF : (half + 1) * E_HALF].rearrange(
                    "(p t) e -> p t e", t=PACK
                ),
            )
            raw2[q] = raw

        def regroup_w1(k, h, copy, skip=0):
            if k not in grouped1:
                grouped1[k] = w1_pool.tile([P, PACK, P, PACK], BF16, name="grouped1", align_bytes=64)
            copy(
                out=grouped1[k][:, :, h * HALF_P + skip : (h + 1) * HALF_P, :].rearrange("p t m j -> p m j t"),
                in_=raw1[k][:, h, :, skip * PACK : F].rearrange("p j (m t) -> p m j t", t=PACK),
            )

        def interleave_w1(k, columns_m):
            if k not in grouped1:
                grouped1[k] = w1_pool.tile([P, PACK, P, PACK], BF16, name="grouped1", align_bytes=64)
            bank = psum.tile([P, PACK, columns_m, PACK], BF16, name="interleaved", tag="bank")
            columns = raw1[k][:, 1, :, :].rearrange("p j (m t) -> p m j t", t=PACK)
            for first in range(0, columns_m, HALF_P // 2):
                span = slice(first, first + HALF_P // 2)
                nc.tensor.matmul(
                    out=bank[:, :, span, :].rearrange("p t m j -> p m j t"),
                    lhsT=identity_bf[:],
                    rhs=columns[:, span, :, :],
                    start=True,
                    stop=True,
                )
            nc.scalar.copy(
                out=grouped1[k][:, :, HALF_P : HALF_P + columns_m, :].rearrange("p t m j -> p t (m j)"),
                in_=bank[:].rearrange("p t m j -> p t (m j)"),
            )

        def quantise_w1(k):
            codes = w1_pool.tile([P, K_PASS], U32, name="codes1", align_bytes=64)
            scales = w1_pool.tile([P, K_PASS], U8, name="scales1", align_bytes=64)
            nc.vector.quantize_mx(
                out=codes[:].bitcast(FP8X4),
                scales=scales[:],
                in_=grouped1[k][:].rearrange("p t m j -> p (t m j)"),
            )
            mx1[k] = (codes, scales)

        def first_matmul(g):
            banks = []
            for t in range(PACK):
                bank = psum.tile([P, TOKENS], F32, name="pre", tag="bank")
                block = slice(t * P, (t + 1) * P)
                for c in range(D_PASSES):
                    codes, scales = mx1[g * D_PASSES + c]
                    nc.tensor.matmul_mx(
                        out=bank[:],
                        lhsT=codes[:, block].bitcast(FP8X4),
                        lhsT_scale=scales[:, block],
                        rhs=x_codes[:, c, :].bitcast(FP8X4),
                        rhs_scale=x_scales[:, c, :],
                        start=(c == 0),
                        stop=(c == D_PASSES - 1),
                    )
                banks.append(bank)
            pre_banks[g] = banks

        def spread_probs(g):
            bank = psum.tile([P, TOKENS], F32, name="spread", tag="bank")
            nc.tensor.matmul(
                out=bank[:],
                lhsT=part_of_partition[:, 2 * g : 2 * g + 2, :].rearrange("p l i -> p (l i)"),
                rhs=leaf_parts[:],
                start=True,
                stop=True,
            )
            nc.scalar.copy(out=probs[:, g, :], in_=bank[:])

        def spread_first_probs():
            bank = psum.tile([P, TOKEN_BLOCKS, P], F32, name="spread", tag="bank")
            for b in range(TOKEN_BLOCKS):
                nc.tensor.transpose(bank[:, b, :], repeated[:, b, :], identity[:])
            nc.scalar.copy(out=probs[:, 0, :], in_=bank[:].rearrange("p b n -> p (b n)"))

        def bias_and_gate(g):
            z = hidden_pool.tile([P, PACK, TOKENS], BF16, name="gated")
            for t in range(PACK):
                nc.vector.scalar_tensor_tensor(
                    out=z[:, t, :],
                    in0=pre_banks[g][t][:],
                    scalar=bias[:, g * PACK + t : g * PACK + t + 1],
                    in1=probs[:, g, :],
                    op0=ADD,
                    op1=MULT,
                )
            gated[g] = z

        def relu_regroup(g):
            h = hidden_pool.tile([P, TOKENS, PACK], BF16, name="hidden", align_bytes=64)
            cut = RELU_CUT if g > 0 else TOKENS
            nc.vector.tensor_scalar_max(
                out=h[:, 0:cut, :].rearrange("p (n i) t -> p n t i", i=RUN),
                in0=gated[g][:, :, 0:cut].rearrange("p t (n i) -> p n t i", i=RUN),
                scalar1=0.0,
            )
            if cut < TOKENS:
                nc.scalar.activation(
                    out=h[:, cut:TOKENS, :].rearrange("p (n i) t -> p n t i", i=RUN),
                    in_=gated[g][:, :, cut:TOKENS].rearrange("p t (n i) -> p n t i", i=RUN),
                    func=RELU,
                )
            hidden[g] = h

        def quantise_h(g):
            nc.vector.quantize_mx(
                out=h_codes[:, g, :].bitcast(FP8X4),
                scales=h_scales[:, g, :],
                in_=hidden[g][:].rearrange("p n t -> p (n t)"),
            )

        with tc.tile_pool(name="setup", bufs=1) as setup:
            warm = setup.tile([P, 1], F32)
            nc.vector.memset(warm[:], 0.0)
            zeros = setup.tile([P, TOKENS], BF16)
            nc.vector.memset(zeros[:], 0.0)

            def keep_busy(times):
                idle = psum.tile([P, TOKENS], F32, name="idle", tag="bank")
                for i in range(times):
                    nc.tensor.matmul(out=idle[:], lhsT=zeros[:, 0:P], rhs=zeros[:], start=True, stop=True)

            logits = setup.tile([P, TOKEN_BLOCKS, NODES], BF16)
            nc.scalar.dma_start(out=logits[:], in_=logit_rows.rearrange("(b p) n -> p b n", p=P))
            node_bias = setup.tile([P, NODES], BF16)
            nc.scalar.dma_start(out=node_bias[:], in_=node_b.partition_broadcast(P))
            b1_bf = setup.tile([P, PAIRS, PACK], BF16)
            nc.scalar.dma_start(
                out=b1_bf[:],
                in_=b1.rearrange("l f -> (l f)").rearrange("(g p t) -> p g t", g=PAIRS, p=P),
            )
            nc.scalar.activation(out=warm[:], in_=warm[:], func=SIGMOID)
            make_identity(nc, identity[:])
            make_identity(nc, identity_bf[:])
            parts = keep.tile([P, TOKEN_BLOCKS, P], BF16)
            nc.gpsimd.memset(parts[:], 0.0)
            leaf_of_row = setup.tile([P, 2, LEAVES], F32)
            nc.gpsimd.tensor_tensor(out=leaf_of_row[:, 0, :], in0=identity[:, 0:LEAVES], in1=identity[:, LEAVES : 2 * LEAVES], op=ADD)
            nc.gpsimd.tensor_tensor(out=leaf_of_row[:, 1, :], in0=leaf_of_row[:, 0, :], in1=identity[:, 2 * LEAVES : PARTS * LEAVES], op=ADD)
            nc.gpsimd.tensor_scalar(
                out=part_of_partition[:],
                in0=leaf_of_row[:, 1, :].unsqueeze(2).to_broadcast([P, LEAVES, HALF_P]),
                scalar1=1.0,
                scalar2=0.0,
                op0=MULT,
                op1=ADD,
            )
            load_w1(0)
            x_blocks = []
            for b in range(TOKEN_BLOCKS):
                x_block = setup.tile([P, D], BF16, name="x%d" % b)
                nc.sync.dma_start(out=x_block[:], in_=x_rows[b * P : (b + 1) * P, :])
                x_blocks.append(x_block)
            for k in range(1, 4):
                load_w1(k)
            load_w2(0)
            for k in range(4, RAW1_BUFS):
                load_w1(k)

            regroup_w1(0, 0, nc.vector.tensor_copy)
            regroup_w1(0, 1, nc.scalar.copy)

            gate_in = setup.tile([P, TOKEN_BLOCKS, NODES], F32)
            nc.vector.tensor_tensor(
                out=gate_in[:],
                in0=logits[:],
                in1=node_bias[:].unsqueeze(1).to_broadcast([P, TOKEN_BLOCKS, NODES]),
                op=ADD,
            )
            gates = setup.tile([P, TOKEN_BLOCKS, NODES, 2], F32)
            nc.scalar.activation(out=gates[:, :, :, 0], in_=gate_in[:], func=SIGMOID)
            nc.scalar.activation(out=gates[:, :, :, 1], in_=gate_in[:], func=SIGMOID, scale=-1.0)

            def tree_level(m, level):
                nodes = 2**m
                children = keep.tile([P, TOKEN_BLOCKS, 2 * nodes], F32, name="level%d" % m)[:]
                nc.gpsimd.tensor_tensor(
                    out=children.rearrange("p b (n s) -> p b n s", s=2),
                    in0=level.unsqueeze(3).to_broadcast([P, TOKEN_BLOCKS, nodes, 2]),
                    in1=gates[:, :, nodes - 1 : 2 * nodes - 1, :],
                    op=MULT,
                )
                return children

            x_grouped = {}

            def turn_x(b, copy):
                words = x_blocks[b][:].bitcast(F32)
                x_turned = psum.tile([P, D_PASSES, 2, P], F32, name="x_turned", tag="bank")
                for c in range(D_PASSES):
                    for u in range(2):
                        first = c * (K_PASS // 2) + u
                        nc.tensor.transpose(
                            x_turned[:, c, u, :], words[:, first : (c + 1) * (K_PASS // 2) : 2], identity[:]
                        )
                grouped = setup.tile([P, D_PASSES, P * PACK], BF16, name="x_grouped%d" % b, align_bytes=64)
                copy(
                    out=grouped[:].bitcast(F32).rearrange("p c (n u) -> p c n u", u=2),
                    in_=x_turned[:].rearrange("p c u n -> p c n u"),
                )
                x_grouped[b] = grouped

            def round_part(s, rest):
                nc.vector.tensor_copy(out=parts[:, :, s * LEAVES : (s + 1) * LEAVES], in_=rest)

            def take_part(s, rest):
                left = keep.tile([P, TOKEN_BLOCKS, LEAVES], F32, name="left%d" % s)[:]
                nc.vector.tensor_tensor(out=left, in0=rest, in1=parts[:, :, s * LEAVES : (s + 1) * LEAVES], op=SUBTRACT)
                return left

            def quantise_x(b):
                for c in range(D_PASSES):
                    nc.vector.quantize_mx(
                        out=x_codes[:, c, b * P : (b + 1) * P].bitcast(FP8X4),
                        scales=x_scales[:, c, b * P : (b + 1) * P],
                        in_=x_grouped[b][:, c, :],
                    )

            level = gates[:, :, 0, :]
            for m in range(1, DEPTH):
                level = tree_level(m, level)
            quantise_w1(0)
            keep_busy(4)
            turn_x(0, nc.vector.tensor_copy)
            keep_busy(1)
            turn_x(1, nc.scalar.copy)
            keep_busy(1)
            repeated = keep.tile([P, TOKEN_BLOCKS, P], F32)
            nc.vector.tensor_copy(
                out=repeated[:].rearrange("p b (l i) -> p b l i", l=2),
                in_=level[:, :, 0:2].unsqueeze(3).to_broadcast([P, TOKEN_BLOCKS, 2, HALF_P]),
            )
            quantise_x(0)
            turn_x(2, nc.vector.tensor_copy)
            quantise_x(1)
            keep_busy(1)
            turn_x(3, nc.scalar.copy)
            keep_busy(2)
            quantise_x(2)
            regroup_w1(1, 0, nc.vector.tensor_copy)
            regroup_w1(1, 1, nc.scalar.copy)
            quantise_x(3)
            quantise_w1(1)
            spread_first_probs()
            first_matmul(0)
            nc.vector.tensor_copy(out=bias[:], in_=b1_bf[:].rearrange("p g t -> p (g t)"))
            round_part(0, level)
            regroup_w1(2, 1, nc.scalar.copy)
            regroup_w1(2, 0, nc.vector.tensor_copy)
            level = take_part(0, level)
            regroup_w1(3, 1, nc.scalar.copy)
            regroup_w1(3, 0, nc.vector.tensor_copy)
            round_part(1, level)
            level = take_part(1, level)
            round_part(2, level)
            regroup_w1(4, 0, nc.scalar.copy)
            parts_turned = psum.tile([P, TOKEN_BLOCKS, P], BF16, name="parts_turned", tag="bank")
            for b in range(TOKEN_BLOCKS):
                nc.tensor.transpose(parts_turned[:, b, :], parts[:, b, :], identity_bf[:])
            nc.scalar.copy(out=leaf_parts[:], in_=parts_turned[:].rearrange("p b n -> p (b n)"))

        w2_pool = stack.enter_context(tc.tile_pool(name="w2", bufs=4))
        out_pool = stack.enter_context(tc.tile_pool(name="out", bufs=TOKEN_BLOCKS))

        def regroup_w2(q, first, last, copy):
            if q >= PAIRS and first == 0:
                grouped2[q] = w2_pool.tile([P, E_HALF, PACK], BF16, name="grouped2", align_bytes=64, bufs=6)
            copy(
                out=grouped2[q][:, first:last, :].rearrange("p (n i) t -> p n t i", i=RUN),
                in_=raw2[q][:, :, first:last].rearrange("p t (n i) -> p n t i", i=RUN),
            )

        def release_gpsimd(q):
            grouped2[q] = w2_pool.tile([P, E_HALF, PACK], BF16, name="grouped2", align_bytes=64, bufs=6)
            nc.vector.memset(grouped2[q][:, 0, 0:1], 0.0)

        def regroup_w2_gpsimd(q, last):
            nc.gpsimd.tensor_scalar(
                out=grouped2[q][:, 0:last, :],
                in0=raw2[q][:, :, 0:last].rearrange("p t n -> p n t"),
                scalar1=1.0,
                scalar2=0.0,
                op0=MULT,
                op1=ADD,
            )

        def quantise_w2(q):
            codes = w2_pool.tile([P, E_HALF], U32, name="codes2", align_bytes=64)
            scales = w2_pool.tile([P, E_HALF], U8, name="scales2", align_bytes=64)
            nc.vector.quantize_mx(
                out=codes[:].bitcast(FP8X4),
                scales=scales[:],
                in_=grouped2[q][:].rearrange("p e t -> p (e t)"),
            )
            mx2[q] = (codes, scales)

        def second_matmul(q):
            half, g = divmod(q, PAIRS)
            codes, scales = mx2[q]
            for b in range(TOKEN_BLOCKS):
                if g == 0:
                    sums[(half, b)] = psum.tile([P, E_HALF], F32, name="sums", tag="bank")
                block = slice(b * P, (b + 1) * P)
                nc.tensor.matmul_mx(
                    out=sums[(half, b)][:],
                    lhsT=h_codes[:, g, block].bitcast(FP8X4),
                    lhsT_scale=h_scales[:, g, block],
                    rhs=codes[:].bitcast(FP8X4),
                    rhs_scale=scales[:],
                    start=(g == 0),
                    stop=(g == PAIRS - 1),
                )

        def store(half, b, copy):
            result = out_pool.tile([P, E_HALF], F32, name="result")
            copy(out=result[:], in_=sums[(half, b)][:])
            nc.sync.dma_start(out=out_rows[b * P : (b + 1) * P, half * E_HALF : (half + 1) * E_HALF], in_=result[:])

        for g in range(PAIRS):
            release_gpsimd(g)
            bias_and_gate(g)
            regroup_w2_gpsimd(g, GPSIMD_CUT)
            if g + 1 < PAIRS:
                spread_probs(g + 1)
                load_w2(g + 1)
                if 2 * g + 4 < W1_PIECES:
                    interleave_w1(2 * g + 4, HALF_P)
                    interleave_w1(2 * g + 5, HALF_P // 2)
                quantise_w1(2 * g + 2)
                quantise_w1(2 * g + 3)
                first_matmul(g + 1)
            else:
                quantise_w2(g - 1)
                quantise_w2(PAIRS)
            if g >= 2:
                second_matmul(g - 2)
            relu_regroup(g)
            for k in (2 * g + 4, 2 * g + 5):
                if k < W1_PIECES:
                    if k > 4:
                        regroup_w1(k, 0, nc.scalar.copy)
                    if k % 2 == 1:
                        regroup_w1(k, 1, nc.scalar.copy, HALF_P // 2)
                    if k + 4 < W1_PIECES:
                        load_w1(k + 4)
            if PAIRS - 5 <= g < PAIRS - 1:
                load_w2(2 * g + 2)
                load_w2(2 * g + 3)
            regroup_w2(g, GPSIMD_CUT, E_HALF, nc.scalar.copy)
            if 0 < g < PAIRS - 1:
                quantise_w2(g - 1)
            if g == PAIRS - 2:
                regroup_w2(PAIRS, 0, E_HALF, nc.scalar.copy)
                regroup_w2(PAIRS + 1, 0, E_HALF, nc.scalar.copy)
            if g == PAIRS - 1:
                quantise_w2(PAIRS + 1)
                quantise_w2(PAIRS - 1)
            quantise_h(g)
        regroup_w2(PAIRS + 2, 0, E_HALF // 2, nc.vector.tensor_copy)
        regroup_w2(PAIRS + 2, E_HALF // 2, E_HALF, nc.scalar.copy)
        second_matmul(PAIRS - 2)
        second_matmul(PAIRS)
        second_matmul(PAIRS + 1)
        second_matmul(PAIRS - 1)

        for q in range(PAIRS + 2, PIECES):
            if q + 1 < PIECES:
                regroup_w2(q + 1, 0, LAST_CUT, nc.vector.tensor_copy)
                regroup_w2(q + 1, LAST_CUT, E_HALF, nc.scalar.copy)
            quantise_w2(q)
            second_matmul(q)
            if q >= PIECES - TOKEN_BLOCKS:
                store(0, q - PIECES + TOKEN_BLOCKS, nc.scalar.copy)
        for b in range(TOKEN_BLOCKS):
            store(1, b, (nc.vector.tensor_copy, nc.scalar.copy)[b % 2])
